import numpy as np
import ml_dtypes


def mxq(x, axis, fmt="e4m3"):
    dtype, down = {"e4m3": (ml_dtypes.float8_e4m3fn, 7), "e5m2": (ml_dtypes.float8_e5m2, 14)}[fmt]
    v = np.moveaxis(np.asarray(x, np.float32).astype(ml_dtypes.bfloat16).astype(np.float64), axis, -1)
    blocks = v.reshape(v.shape[:-1] + (-1, 32))
    amax = np.abs(blocks).max(-1, keepdims=True)
    byte = np.maximum(np.where(amax > 0, np.frexp(amax)[1] - 1 + 127, 0) - down, 1)
    scale = np.exp2(byte - 127.0)
    codes = (blocks / scale).astype(np.float32).astype(dtype).astype(np.float64)
    return np.moveaxis((codes * scale).reshape(v.shape), -1, axis)


WIDE = False


def mx_kscale(k):
    if not WIDE:
        return np.ones(k)
    levels = np.array([10, -10, 5, -5, 0])
    if k % 512:
        return np.exp2(np.random.permutation(np.resize(levels, k // 32))).repeat(32)
    a = np.empty((k // 512, 16))
    for p in range(k // 512):
        a[p, :8] = np.random.permutation(np.resize(levels, 8))
        for g in range(8):
            far = levels[np.abs(levels - a[p, g]) >= 10]
            a[p, g + 8] = far[np.random.randint(len(far))]
    return np.exp2(a.ravel()).repeat(32)


BF16 = ml_dtypes.bfloat16


def bf(x):
    return np.asarray(x, np.float32).astype(BF16)


def f64(x):
    return np.asarray(x).astype(np.float64)


B, L, H, U = 2, 1024, 1024, 1024
R_MIN, R_MAX = 0.9, 0.999


def setup_inputs():
    s, t = mx_kscale(H), mx_kscale(U)
    inputs = np.random.standard_normal((B, L, H)) * s
    Wi = np.random.standard_normal((U, H)) / np.sqrt(H) / s[None, :] * t[:, None]
    bi = np.random.standard_normal(U) * 0.03 * t
    Wo = np.random.standard_normal((H, U)) / np.sqrt(U) / t[None, :]
    bo = np.random.standard_normal(H) * 0.1
    r = np.random.uniform(size=U)
    nu_log = np.log(-0.5 * np.log(r * (R_MAX ** 2 - R_MIN ** 2) + R_MIN ** 2))
    gamma_log = np.log(np.sqrt(1.0 - np.exp(-np.exp(nu_log)) ** 2))
    params_log = np.stack([nu_log, gamma_log])
    return {"inputs": bf(inputs), "Wi": bf(Wi), "bi": bf(bi), "Wo": bf(Wo), "bo": bf(bo), "params_log": bf(params_log)}


def reference(inputs, Wi, bi, Wo, bo, params_log):
    u = (mxq(f64(inputs), 2, "e4m3") @ mxq(f64(Wi), 1, "e4m3").T) + f64(bi)
    params = np.exp(f64(params_log))
    nu, gamma = params[0], params[1]

    log2_L = int(np.ceil(np.log2(L)))
    pad_len = 2 ** log2_L - L
    x = np.pad(u, ((0, 0), (0, pad_len), (0, 0))) if pad_len else u
    Lp = 2 ** log2_L

    for i in range(1, log2_L + 1):
        l = 2 ** i
        x = x.reshape(B * Lp // l, l, U)
        x1, x2 = x[:, : l // 2], x[:, l // 2:]
        pos = np.arange(1, l // 2 + 1, dtype=np.float64)
        lambs = np.exp(-pos[:, None] * nu)
        x2 = x2 + lambs * x1[:, -1:]
        x = np.concatenate([x1, x2], axis=1).reshape(B, Lp, U)

    x = x[:, :L] * gamma
    return (mxq(x, 2, "e4m3") @ mxq(f64(Wo), 1, "e4m3").T) + f64(bo)

@@ -1,0 +1,250 @@
+from contextlib import ExitStack
+
+import concourse.bass as bass
+import concourse.mybir as mybir
+import concourse.tile as tile
+from concourse.masks import make_identity
+
+F32 = mybir.dt.float32
+BF16 = mybir.dt.bfloat16
+U32 = mybir.dt.uint32
+U8 = mybir.dt.uint8
+FP8X4 = mybir.dt.float8_e4m3fn_x4
+ACTF = mybir.ActivationFunctionType
+ALU = mybir.AluOpType
+
+P = 128
+TOK = 2048
+SEQ = 1024
+H = 1024
+U = 1024
+CH = 512
+NCH = TOK // CH
+
+FLOPS = 2 * 2 * TOK * H * U
+
+
+def tile_slru_kernel(tc, inputs, Wi, bi, Wo, bo, params_log, out):
+    nc = tc.nc
+    x_in = inputs.flatten_outer_dims()
+    o_out = out.flatten_outer_dims()
+    with ExitStack() as ctx:
+        const = ctx.enter_context(tc.tile_pool(name="const", bufs=1))
+        rawp = ctx.enter_context(tc.tile_pool(name="raw", bufs=1))
+        keep = ctx.enter_context(tc.tile_pool(name="keep", bufs=1))
+        stg = ctx.enter_context(tc.tile_pool(name="stg", bufs=2))
+        vpool = ctx.enter_context(tc.tile_pool(name="vp", bufs=8))
+        xpool = ctx.enter_context(tc.tile_pool(name="xp", bufs=4))
+        gpool = ctx.enter_context(tc.tile_pool(name="gp", bufs=2))
+        opool = ctx.enter_context(tc.tile_pool(name="op", bufs=4))
+        ps_t = ctx.enter_context(tc.psum_pool(name="pst", bufs=2))
+        ps_1 = ctx.enter_context(tc.psum_pool(name="ps1", bufs=3))
+        ps_2 = ctx.enter_context(tc.psum_pool(name="ps2", bufs=2))
+        ps_c = ctx.enter_context(tc.psum_pool(name="psc", bufs=1))
+
+        in_raw = []
+        for c in range(NCH):
+            t = rawp.tile([P, 4, H], BF16, name="in_raw%d" % c)
+            in_raw.append(t)
+        wi_raw = []
+        for a in range(2):
+            t = rawp.tile([P, 4, H], BF16, name="wi_raw%d" % a)
+            wi_raw.append(t)
+        wo_raw = []
+        for h in range(2):
+            t = rawp.tile([P, 4, U], BF16, name="wo_raw%d" % h)
+            wo_raw.append(t)
+
+        pl = [const.tile([P, 8], BF16, name="pl%d" % r) for r in range(2)]
+        bi_b = const.tile([P, 8], BF16, name="bi_b")
+        for r in range(2):
+            nc.scalar.dma_start(
+                out=pl[r][:].rearrange("m (a e) -> m a e", e=4),
+                in_=params_log[r].rearrange("(a m e) -> m a e", a=2, e=4),
+            )
+        nc.scalar.dma_start(
+            out=bi_b[:].rearrange("m (a e) -> m a e", e=4),
+            in_=bi.rearrange("(a m e) -> m a e", a=2, e=4),
+        )
+
+        def load_in(c, split):
+            src = x_in[c * CH : (c + 1) * CH, :].rearrange("(i p) h -> p i h", p=P)
+            if split:
+                for i in range(4):
+                    nc.sync.dma_start(out=in_raw[c][:, i, :], in_=src[:, i, :])
+            else:
+                nc.sync.dma_start(out=in_raw[c][:], in_=src)
+
+        def load_wi(a):
+            nc.sync.dma_start(
+                out=wi_raw[a][:],
+                in_=Wi[a * 512 : (a + 1) * 512, :].rearrange("(m e) h -> m e h", e=4),
+            )
+
+        def load_wo(h):
+            nc.sync.dma_start(
+                out=wo_raw[h][:],
+                in_=Wo[h * 512 : (h + 1) * 512, :].rearrange("(i p) u -> p i u", p=P),
+            )
+
+        load_in(0, True)
+        for a in range(2):
+            load_wi(a)
+        load_in(1, False)
+        load_wo(0)
+        load_wo(1)
+        load_in(2, False)
+        load_in(3, False)
+
+        bo_b = const.tile([P, H], BF16, name="bo_b")
+        nc.gpsimd.dma_start(out=bo_b[:], in_=bo.partition_broadcast(P))
+
+        ident = const.tile([P, P], F32, name="ident")
+        make_identity(nc, ident[:])
+
+        nu = const.tile([P, 8], F32, name="nu")
+        lam = const.tile([P, 8], F32, name="lam")
+        gam = const.tile([P, 8], F32, name="gam")
+        gb = const.tile([P, 8], F32, name="gb")
+        bi_f = const.tile([P, 8], F32, name="bi_f")
+        nc.scalar.activation(out=nu[:], in_=pl[0][:], func=ACTF.Exp)
+        nc.scalar.activation(out=lam[:], in_=nu[:], func=ACTF.Exp, scale=-1.0)
+        lam_p = ps_c.tile([P, 8], F32, name="lam_p")
+        nc.tensor.matmul(out=lam_p[:], lhsT=ident[:], rhs=lam[:], start=True, stop=True)
+        nc.scalar.activation(out=gam[:], in_=pl[1][:], func=ACTF.Exp)
+        nc.vector.tensor_copy(out=bi_f[:], in_=bi_b[:])
+        nc.vector.tensor_tensor(out=gb[:], in0=gam[:], in1=bi_f[:], op=ALU.mult)
+
+        bo_f = const.tile([P, H], F32, name="bo_f")
+        nc.gpsimd.tensor_scalar(
+            out=bo_f[:], in0=bo_b[:], scalar1=1.0, scalar2=0.0, op0=ALU.mult, op1=ALU.add
+        )
+
+        def codes_pair(nm):
+            cd = keep.tile([P, 2, 512], U32, name=nm + "_c", align_bytes=64)
+            sc = keep.tile([P, 2, 512], U8, name=nm + "_s", align_bytes=64)
+            return cd, sc
+
+        in_q = [codes_pair("inq%d" % c) for c in range(NCH)]
+        wi_q = [codes_pair("wiq%d" % g) for g in range(2)]
+        wo_q = [codes_pair("woq%d" % h) for h in range(2)]
+        x_q = [codes_pair("xq%d" % c) for c in range(NCH)]
+
+        def tq_block(raws, q):
+            stage = stg.tile([P, 2, 512, 2], F32, name="stage", align_bytes=64)
+            for i in range(4):
+                bank = ps_t.tile([P, 2, 2, P], F32, name="bank")
+                words = raws[i].bitcast(F32)
+                for g in range(2):
+                    for u in range(2):
+                        nc.tensor.transpose(
+                            bank[:, g, u, :], words[:, 256 * g + u : 256 * (g + 1) : 2], ident[:]
+                        )
+                nc.scalar.copy(
+                    out=stage[:, :, 128 * i : 128 * (i + 1), :],
+                    in_=bank[:].rearrange("p g u c -> p g c u"),
+                )
+            nc.vector.quantize_mx(
+                out=q[0][:].rearrange("p g c -> p (g c)").bitcast(FP8X4),
+                scales=q[1][:].rearrange("p g c -> p (g c)"),
+                in_=stage[:].rearrange("p g c u -> p (g c u)").bitcast(BF16),
+            )
+
+        xs_prev = [None, None]
+
+        def stage1(c, g2):
+            xs = xpool.tile([P, 4, CH], F32, name="xs")
+            first = (c * CH) % SEQ == 0
+            for j in range(4):
+                ct = 4 * g2 + j
+                acc = ps_1.tile([P, CH], F32, name="acc1")
+                for g in range(2):
+                    nc.tensor.matmul_mx(
+                        out=acc[:],
+                        lhsT=wi_q[g2][0][:, g, 128 * j : 128 * (j + 1)].bitcast(FP8X4),
+                        lhsT_scale=wi_q[g2][1][:, g, 128 * j : 128 * (j + 1)],
+                        rhs=in_q[c][0][:, g, :].bitcast(FP8X4),
+                        rhs_scale=in_q[c][1][:, g, :],
+                        start=(g == 0),
+                        stop=(g == 1),
+                    )
+                v = vpool.tile([P, CH], F32, name="v")
+                nc.scalar.activation(
+                    out=v[:],
+                    in_=acc[:],
+                    func=ACTF.Identity,
+                    scale=gam[:, ct : ct + 1],
+                    bias=gb[:, ct : ct + 1],
+                )
+                init = 0.0 if first else xs_prev[g2][:, j, CH - 1 : CH]
+                nc.vector.tensor_tensor_scan(
+                    out=xs[:, j, :],
+                    data0=lam_p[:, ct : ct + 1].to_broadcast([P, CH]),
+                    data1=v[:],
+                    initial=init,
+                    op0=ALU.mult,
+                    op1=ALU.add,
+                )
+            xs_prev[g2] = xs
+            gx = gpool.tile([P, CH, 4], BF16, name="gx", align_bytes=64)
+            nc.gpsimd.tensor_scalar(
+                out=gx[:],
+                in0=xs[:].rearrange("p j t -> p t j"),
+                scalar1=1.0,
+                scalar2=0.0,
+                op0=ALU.mult,
+                op1=ALU.add,
+            )
+            nc.vector.quantize_mx(
+                out=x_q[c][0][:, g2, :].bitcast(FP8X4),
+                scales=x_q[c][1][:, g2, :],
+                in_=gx[:].rearrange("p t j -> p (t j)"),
+            )
+
+        def stage2(c):
+            for i in range(4):
+                o = opool.tile([P, H], F32, name="o")
+                for h in range(2):
+                    acc = ps_2.tile([P, 512], F32, name="acc2")
+                    for g in range(2):
+                        nc.tensor.matmul_mx(
+                            out=acc[:],
+                            lhsT=x_q[c][0][:, g, 128 * i : 128 * (i + 1)].bitcast(FP8X4),
+                            lhsT_scale=x_q[c][1][:, g, 128 * i : 128 * (i + 1)],
+                            rhs=wo_q[h][0][:, g, :].bitcast(FP8X4),
+                            rhs_scale=wo_q[h][1][:, g, :],
+                            start=(g == 0),
+                            stop=(g == 1),
+                        )
+                    hs = slice(512 * h, 512 * (h + 1))
+                    if h == 1 and i % 2 == 1:
+                        nc.vector.tensor_tensor(out=o[:, hs], in0=acc[:], in1=bo_f[:, hs], op=ALU.add)
+                    else:
+                        nc.scalar.copy(out=o[:, hs], in_=acc[:])
+                        nc.gpsimd.tensor_tensor(out=o[:, hs], in0=o[:, hs], in1=bo_f[:, hs], op=ALU.add)
+                r0 = c * CH + i * P
+                nc.sync.dma_start(out=o_out[r0 : r0 + P, :], in_=o[:])
+
+        def wi_views(g2):
+            return [wi_raw[g2][:, e, :] for e in range(4)]
+
+        tq_block([in_raw[0][:, i, :] for i in range(4)], in_q[0])
+        tq_block(wi_views(0), wi_q[0])
+        stage1(0, 0)
+        tq_block(wi_views(1), wi_q[1])
+        stage1(0, 1)
+        tq_block([in_raw[1][:, i, :] for i in range(4)], in_q[1])
+        stage1(1, 0)
+        stage1(1, 1)
+        tq_block([wo_raw[0][:, i, :] for i in range(4)], wo_q[0])
+        tq_block([wo_raw[1][:, i, :] for i in range(4)], wo_q[1])
+        stage2(0)
+        tq_block([in_raw[2][:, i, :] for i in range(4)], in_q[2])
+        stage1(2, 0)
+        stage1(2, 1)
+        stage2(1)
+        tq_block([in_raw[3][:, i, :] for i in range(4)], in_q[3])
+        stage1(3, 0)
+        stage1(3, 1)
+        stage2(2)
+        stage2(3)

@@ -33,27 +33,39 @@ def tile_slru_kernel(tc, inputs, Wi, bi, Wo, bo, params_log, out):
         rawp = ctx.enter_context(tc.tile_pool(name="raw", bufs=1))
         keep = ctx.enter_context(tc.tile_pool(name="keep", bufs=1))
         stg = ctx.enter_context(tc.tile_pool(name="stg", bufs=2))
-        vpool = ctx.enter_context(tc.tile_pool(name="vp", bufs=8))
-        xpool = ctx.enter_context(tc.tile_pool(name="xp", bufs=4))
+        vpool = ctx.enter_context(tc.tile_pool(name="vp", bufs=6))
+        xpool = ctx.enter_context(tc.tile_pool(name="xp", bufs=3))
         gpool = ctx.enter_context(tc.tile_pool(name="gp", bufs=2))
-        opool = ctx.enter_context(tc.tile_pool(name="op", bufs=4))
-        ps_t = ctx.enter_context(tc.psum_pool(name="pst", bufs=2))
-        ps_1 = ctx.enter_context(tc.psum_pool(name="ps1", bufs=3))
+        opool = ctx.enter_context(tc.tile_pool(name="op", bufs=6))
+        ps_t = ctx.enter_context(tc.psum_pool(name="pst", bufs=3))
+        ps_1 = ctx.enter_context(tc.psum_pool(name="ps1", bufs=2))
         ps_2 = ctx.enter_context(tc.psum_pool(name="ps2", bufs=2))
         ps_c = ctx.enter_context(tc.psum_pool(name="psc", bufs=1))
+        ctx.enter_context(tc.manual_schedule())
 
-        in_raw = []
-        for c in range(NCH):
-            t = rawp.tile([P, 4, H], BF16, name="in_raw%d" % c)
-            in_raw.append(t)
-        wi_raw = []
-        for a in range(2):
-            t = rawp.tile([P, 4, H], BF16, name="wi_raw%d" % a)
-            wi_raw.append(t)
-        wo_raw = []
-        for h in range(2):
-            t = rawp.tile([P, 4, U], BF16, name="wo_raw%d" % h)
-            wo_raw.append(t)
+        ident = const.tile([P, P], F32, name="ident")
+        make_identity(nc, ident[:])
+
+        raw = {}
+        for nm in ("in0", "in1", "in2", "in3", "wi0", "wi1", "wo0", "wo1"):
+            t = rawp.tile([P, 4, H], BF16, name="raw_" + nm)
+            raw[nm] = t
+
+        def source(nm):
+            i = int(nm[2])
+            if nm[:2] == "in":
+                return x_in[i * CH : (i + 1) * CH, :].rearrange("(i p) h -> p i h", p=P)
+            if nm[:2] == "wi":
+                return Wi[i * 512 : (i + 1) * 512, :].rearrange("(m e) h -> m e h", e=4)
+            return Wo[i * 512 : (i + 1) * 512, :].rearrange("(i p) u -> p i u", p=P)
+
+        def load(nm, pieces):
+            src = source(nm)
+            n = 4 // pieces
+            for i in range(pieces):
+                nc.sync.dma_start(
+                    out=raw[nm][:, n * i : n * (i + 1), :], in_=src[:, n * i : n * (i + 1), :]
+                )
 
         pl = [const.tile([P, 8], BF16, name="pl%d" % r) for r in range(2)]
         bi_b = const.tile([P, 8], BF16, name="bi_b")
@@ -66,185 +78,299 @@ def tile_slru_kernel(tc, inputs, Wi, bi, Wo, bo, params_log, out):
             out=bi_b[:].rearrange("m (a e) -> m a e", e=4),
             in_=bi.rearrange("(a m e) -> m a e", a=2, e=4),
         )
-
-        def load_in(c, split):
-            src = x_in[c * CH : (c + 1) * CH, :].rearrange("(i p) h -> p i h", p=P)
-            if split:
-                for i in range(4):
-                    nc.sync.dma_start(out=in_raw[c][:, i, :], in_=src[:, i, :])
-            else:
-                nc.sync.dma_start(out=in_raw[c][:], in_=src)
-
-        def load_wi(a):
-            nc.sync.dma_start(
-                out=wi_raw[a][:],
-                in_=Wi[a * 512 : (a + 1) * 512, :].rearrange("(m e) h -> m e h", e=4),
-            )
-
-        def load_wo(h):
-            nc.sync.dma_start(
-                out=wo_raw[h][:],
-                in_=Wo[h * 512 : (h + 1) * 512, :].rearrange("(i p) u -> p i u", p=P),
-            )
-
-        load_in(0, True)
-        for a in range(2):
-            load_wi(a)
-        load_in(1, False)
-        load_wo(0)
-        load_wo(1)
-        load_in(2, False)
-        load_in(3, False)
-
+        load("in0", 4)
+        load("wi0", 4)
+        load("wi1", 2)
+        load("in1", 2)
+        load("wo0", 1)
+        load("wo1", 1)
         bo_b = const.tile([P, H], BF16, name="bo_b")
-        nc.gpsimd.dma_start(out=bo_b[:], in_=bo.partition_broadcast(P))
-
-        ident = const.tile([P, P], F32, name="ident")
-        make_identity(nc, ident[:])
+        nc.sync.dma_start(out=bo_b[:], in_=bo.partition_broadcast(P))
+        load("in2", 1)
+        load("in3", 1)
 
         nu = const.tile([P, 8], F32, name="nu")
         lam = const.tile([P, 8], F32, name="lam")
         gam = const.tile([P, 8], F32, name="gam")
         gb = const.tile([P, 8], F32, name="gb")
         bi_f = const.tile([P, 8], F32, name="bi_f")
-        nc.scalar.activation(out=nu[:], in_=pl[0][:], func=ACTF.Exp)
-        nc.scalar.activation(out=lam[:], in_=nu[:], func=ACTF.Exp, scale=-1.0)
         lam_p = ps_c.tile([P, 8], F32, name="lam_p")
-        nc.tensor.matmul(out=lam_p[:], lhsT=ident[:], rhs=lam[:], start=True, stop=True)
-        nc.scalar.activation(out=gam[:], in_=pl[1][:], func=ACTF.Exp)
-        nc.vector.tensor_copy(out=bi_f[:], in_=bi_b[:])
-        nc.vector.tensor_tensor(out=gb[:], in0=gam[:], in1=bi_f[:], op=ALU.mult)
-
         bo_f = const.tile([P, H], F32, name="bo_f")
-        nc.gpsimd.tensor_scalar(
-            out=bo_f[:], in0=bo_b[:], scalar1=1.0, scalar2=0.0, op0=ALU.mult, op1=ALU.add
-        )
 
-        def codes_pair(nm):
-            cd = keep.tile([P, 2, 512], U32, name=nm + "_c", align_bytes=64)
-            sc = keep.tile([P, 2, 512], U8, name=nm + "_s", align_bytes=64)
-            return cd, sc
+        def constants():
+            nc.scalar.activation(out=nu[:], in_=pl[0][:], func=ACTF.Exp)
+            nc.scalar.activation(out=lam[:], in_=nu[:], func=ACTF.Exp, scale=-1.0)
+            nc.scalar.activation(out=gam[:], in_=pl[1][:], func=ACTF.Exp)
+            nc.vector.tensor_copy(out=bi_f[:], in_=bi_b[:])
+            nc.vector.tensor_tensor(out=gb[:], in0=gam[:], in1=bi_f[:], op=ALU.mult)
 
-        in_q = [codes_pair("inq%d" % c) for c in range(NCH)]
-        wi_q = [codes_pair("wiq%d" % g) for g in range(2)]
-        wo_q = [codes_pair("woq%d" % h) for h in range(2)]
-        x_q = [codes_pair("xq%d" % c) for c in range(NCH)]
+        codes, scales = {}, {}
+        for nm in raw:
+            c_t = keep.tile([P, 1024], U32, name="c_" + nm, align_bytes=64)
+            s_t = keep.tile([P, 1024], U8, name="s_" + nm, align_bytes=64)
+            codes[nm], scales[nm] = c_t, s_t
+        xc, xsc = {}, {}
+        for c in range(NCH):
+            for g in range(2):
+                c_t = keep.tile([P, CH], U32, name="xc%d%d" % (c, g), align_bytes=64)
+                s_t = keep.tile([P, CH], U8, name="xs%d%d" % (c, g), align_bytes=64)
+                xc[c, g], xsc[c, g] = c_t, s_t
 
-        def tq_block(raws, q):
-            stage = stg.tile([P, 2, 512, 2], F32, name="stage", align_bytes=64)
-            for i in range(4):
-                bank = ps_t.tile([P, 2, 2, P], F32, name="bank")
-                words = raws[i].bitcast(F32)
-                for g in range(2):
-                    for u in range(2):
-                        nc.tensor.transpose(
-                            bank[:, g, u, :], words[:, 256 * g + u : 256 * (g + 1) : 2], ident[:]
-                        )
-                nc.scalar.copy(
-                    out=stage[:, :, 128 * i : 128 * (i + 1), :],
-                    in_=bank[:].rearrange("p g u c -> p g c u"),
+        stages = {}
+
+        def turn(nm, i, on_vector=False):
+            if i == 0:
+                stage = stg.tile([P, 2048], F32, name="stage", align_bytes=64)
+                stages[nm] = stage
+            bank = ps_t.tile([P, 2, 2, P], F32, name="bank")
+            words = raw[nm][:, i, :].bitcast(F32)
+            for g in range(2):
+                for u in range(2):
+                    nc.tensor.transpose(
+                        bank[:, g, u, :], words[:, 256 * g + u : 256 * (g + 1) : 2], ident[:]
+                    )
+            if nm[:2] == "wi":
+                dst = stages[nm][:, 512 * i : 512 * (i + 1)].rearrange(
+                    "p (g c u) -> p g c u", g=2, u=2
                 )
+            else:
+                dst = stages[nm][:].rearrange("p (g c u) -> p g c u", g=2, u=2)[
+                    :, :, P * i : P * (i + 1), :
+                ]
+            src = bank[:].rearrange("p g u c -> p g c u")
+            if on_vector:
+                nc.vector.tensor_copy(out=dst, in_=src)
+            else:
+                nc.scalar.copy(out=dst, in_=src)
+
+        def quant(nm, lo, n):
             nc.vector.quantize_mx(
-                out=q[0][:].rearrange("p g c -> p (g c)").bitcast(FP8X4),
-                scales=q[1][:].rearrange("p g c -> p (g c)"),
-                in_=stage[:].rearrange("p g c u -> p (g c u)").bitcast(BF16),
+                out=codes[nm][:, lo : lo + n].bitcast(FP8X4),
+                scales=scales[nm][:, lo : lo + n],
+                in_=stages[nm][:, 2 * lo : 2 * (lo + n)].bitcast(BF16),
             )
 
-        xs_prev = [None, None]
+        acc1, vs, xs, gx = {}, {}, {}, {}
 
-        def stage1(c, g2):
-            xs = xpool.tile([P, 4, CH], F32, name="xs")
-            first = (c * CH) % SEQ == 0
-            for j in range(4):
-                ct = 4 * g2 + j
-                acc = ps_1.tile([P, CH], F32, name="acc1")
-                for g in range(2):
-                    nc.tensor.matmul_mx(
-                        out=acc[:],
-                        lhsT=wi_q[g2][0][:, g, 128 * j : 128 * (j + 1)].bitcast(FP8X4),
-                        lhsT_scale=wi_q[g2][1][:, g, 128 * j : 128 * (j + 1)],
-                        rhs=in_q[c][0][:, g, :].bitcast(FP8X4),
-                        rhs_scale=in_q[c][1][:, g, :],
-                        start=(g == 0),
-                        stop=(g == 1),
-                    )
-                v = vpool.tile([P, CH], F32, name="v")
-                nc.scalar.activation(
-                    out=v[:],
-                    in_=acc[:],
-                    func=ACTF.Identity,
-                    scale=gam[:, ct : ct + 1],
-                    bias=gb[:, ct : ct + 1],
+        def first(u, j):
+            c, g2 = u // 2, u % 2
+            ct = 4 * g2 + j
+            acc = ps_1.tile([P, CH], F32, name="acc1")
+            wi, xi = "wi%d" % g2, "in%d" % c
+            for g in range(2):
+                w = slice(256 * j + 128 * g, 256 * j + 128 * (g + 1))
+                r = slice(512 * g, 512 * (g + 1))
+                nc.tensor.matmul_mx(
+                    out=acc[:],
+                    lhsT=codes[wi][:, w].bitcast(FP8X4),
+                    lhsT_scale=scales[wi][:, w],
+                    rhs=codes[xi][:, r].bitcast(FP8X4),
+                    rhs_scale=scales[xi][:, r],
+                    start=(g == 0),
+                    stop=(g == 1),
                 )
-                init = 0.0 if first else xs_prev[g2][:, j, CH - 1 : CH]
-                nc.vector.tensor_tensor_scan(
-                    out=xs[:, j, :],
-                    data0=lam_p[:, ct : ct + 1].to_broadcast([P, CH]),
-                    data1=v[:],
-                    initial=init,
-                    op0=ALU.mult,
-                    op1=ALU.add,
-                )
-            xs_prev[g2] = xs
-            gx = gpool.tile([P, CH, 4], BF16, name="gx", align_bytes=64)
-            nc.gpsimd.tensor_scalar(
-                out=gx[:],
-                in0=xs[:].rearrange("p j t -> p t j"),
-                scalar1=1.0,
-                scalar2=0.0,
+            v = vpool.tile([P, CH], F32, name="v")
+            nc.scalar.activation(
+                out=v[:],
+                in_=acc[:],
+                func=ACTF.Identity,
+                scale=gam[:, ct : ct + 1],
+                bias=gb[:, ct : ct + 1],
+            )
+            vs[u, j] = v
+
+        def scan(u, j):
+            c, g2 = u // 2, u % 2
+            ct = 4 * g2 + j
+            if j == 0:
+                t = xpool.tile([P, 4, CH], F32, name="xs")
+                xs[u] = t
+            init = 0.0 if (c * CH) % SEQ == 0 else xs[u - 2][:, j, CH - 1 : CH]
+            nc.vector.tensor_tensor_scan(
+                out=xs[u][:, j, :],
+                data0=lam_p[:, ct : ct + 1].to_broadcast([P, CH]),
+                data1=vs[u, j][:],
+                initial=init,
                 op0=ALU.mult,
                 op1=ALU.add,
             )
+
+        def weave(u, lo, n, engine):
+            if lo == 0:
+                t = gpool.tile([P, CH, 4], BF16, name="gx", align_bytes=64)
+                gx[u] = t
+            dst = gx[u][:, lo : lo + n, :]
+            src = xs[u][:, :, lo : lo + n].rearrange("p j t -> p t j")
+            if engine == "pool":
+                nc.gpsimd.tensor_scalar(
+                    out=dst, in0=src, scalar1=1.0, scalar2=0.0, op0=ALU.mult, op1=ALU.add
+                )
+            elif engine == "vector":
+                nc.vector.tensor_copy(out=dst, in_=src)
+            else:
+                nc.scalar.copy(out=dst, in_=src)
+
+        def quant_x(u, lo, n):
+            c, g2 = u // 2, u % 2
             nc.vector.quantize_mx(
-                out=x_q[c][0][:, g2, :].bitcast(FP8X4),
-                scales=x_q[c][1][:, g2, :],
-                in_=gx[:].rearrange("p t j -> p (t j)"),
+                out=xc[c, g2][:, lo : lo + n].bitcast(FP8X4),
+                scales=xsc[c, g2][:, lo : lo + n],
+                in_=gx[u][:, lo : lo + n, :].rearrange("p t j -> p (t j)"),
             )
 
-        def stage2(c):
-            for i in range(4):
+        outs = {}
+
+        def second(c, i, h, on_vector):
+            if h == 0:
                 o = opool.tile([P, H], F32, name="o")
-                for h in range(2):
-                    acc = ps_2.tile([P, 512], F32, name="acc2")
-                    for g in range(2):
-                        nc.tensor.matmul_mx(
-                            out=acc[:],
-                            lhsT=x_q[c][0][:, g, 128 * i : 128 * (i + 1)].bitcast(FP8X4),
-                            lhsT_scale=x_q[c][1][:, g, 128 * i : 128 * (i + 1)],
-                            rhs=wo_q[h][0][:, g, :].bitcast(FP8X4),
-                            rhs_scale=wo_q[h][1][:, g, :],
-                            start=(g == 0),
-                            stop=(g == 1),
-                        )
-                    hs = slice(512 * h, 512 * (h + 1))
-                    if h == 1 and i % 2 == 1:
-                        nc.vector.tensor_tensor(out=o[:, hs], in0=acc[:], in1=bo_f[:, hs], op=ALU.add)
-                    else:
-                        nc.scalar.copy(out=o[:, hs], in_=acc[:])
-                        nc.gpsimd.tensor_tensor(out=o[:, hs], in0=o[:, hs], in1=bo_f[:, hs], op=ALU.add)
-                r0 = c * CH + i * P
+                outs[c, i] = o
+            o = outs[c, i]
+            acc = ps_2.tile([P, 512], F32, name="acc2")
+            ts = slice(P * i, P * (i + 1))
+            wo = "wo%d" % h
+            for g in range(2):
+                r = slice(512 * g, 512 * (g + 1))
+                nc.tensor.matmul_mx(
+                    out=acc[:],
+                    lhsT=xc[c, g][:, ts].bitcast(FP8X4),
+                    lhsT_scale=xsc[c, g][:, ts],
+                    rhs=codes[wo][:, r].bitcast(FP8X4),
+                    rhs_scale=scales[wo][:, r],
+                    start=(g == 0),
+                    stop=(g == 1),
+                )
+            hs = slice(512 * h, 512 * (h + 1))
+            if on_vector:
+                nc.vector.tensor_tensor(out=o[:, hs], in0=acc[:], in1=bo_f[:, hs], op=ALU.add)
+            else:
+                nc.scalar.copy(out=o[:, hs], in_=acc[:])
+                nc.gpsimd.tensor_tensor(out=o[:, hs], in0=o[:, hs], in1=bo_f[:, hs], op=ALU.add)
+            r0 = c * CH + i * P
+            if c == 3 and i == 3:
+                nc.sync.dma_start(out=o_out[r0 : r0 + P, hs], in_=o[:, hs])
+            elif h == 1:
                 nc.sync.dma_start(out=o_out[r0 : r0 + P, :], in_=o[:])
 
-        def wi_views(g2):
-            return [wi_raw[g2][:, e, :] for e in range(4)]
-
-        tq_block([in_raw[0][:, i, :] for i in range(4)], in_q[0])
-        tq_block(wi_views(0), wi_q[0])
-        stage1(0, 0)
-        tq_block(wi_views(1), wi_q[1])
-        stage1(0, 1)
-        tq_block([in_raw[1][:, i, :] for i in range(4)], in_q[1])
-        stage1(1, 0)
-        stage1(1, 1)
-        tq_block([wo_raw[0][:, i, :] for i in range(4)], wo_q[0])
-        tq_block([wo_raw[1][:, i, :] for i in range(4)], wo_q[1])
-        stage2(0)
-        tq_block([in_raw[2][:, i, :] for i in range(4)], in_q[2])
-        stage1(2, 0)
-        stage1(2, 1)
-        stage2(1)
-        tq_block([in_raw[3][:, i, :] for i in range(4)], in_q[3])
-        stage1(3, 0)
-        stage1(3, 1)
-        stage2(2)
-        stage2(3)
+        for i in range(4):
+            turn("in0", i, on_vector=(i % 2 == 1))
+            if i == 1:
+                constants()
+            if i % 2 == 1:
+                for g in range(2):
+                    quant("in0", 512 * g + 128 * (i - 1), 256)
+        nc.tensor.matmul(out=lam_p[:], lhsT=ident[:], rhs=lam[:], start=True, stop=True)
+        turn("wi0", 0)
+        turn("wi0", 1, on_vector=True)
+        quant("wi0", 0, 256)
+        turn("wi0", 2)
+        first(0, 0)
+        quant("wi0", 256, 256)
+        turn("wi0", 3, on_vector=True)
+        first(0, 1)
+        quant("wi0", 512, 256)
+        turn("wi1", 0)
+        first(0, 2)
+        scan(0, 0)
+        quant("wi0", 768, 256)
+        turn("wi1", 1, on_vector=True)
+        first(0, 3)
+        scan(0, 1)
+        turn("wi1", 2)
+        quant("wi1", 0, 512)
+        turn("wi1", 3)
+        first(1, 0)
+        scan(0, 2)
+        quant("wi1", 512, 512)
+        first(1, 1)
+        turn("in1", 0)
+        turn("in1", 1)
+        scan(0, 3)
+        weave(0, 0, 256, "pool")
+        weave(0, 256, 256, "pool")
+        first(1, 2)
+        turn("in1", 2)
+        turn("in1", 3)
+        first(1, 3)
+        scan(1, 0)
+        scan(1, 1)
+        quant("in1", 0, 1024)
+        first(2, 0)
+        first(2, 1)
+        turn("wo0", 0)
+        turn("wo0", 1)
+        scan(1, 2)
+        first(2, 2)
+        first(2, 3)
+        turn("wo0", 2)
+        turn("wo0", 3)
+        scan(1, 3)
+        quant_x(0, 0, 512)
+        weave(1, 0, 256, "pool")
+        weave(1, 256, 256, "pool")
+        nc.gpsimd.tensor_scalar(
+            out=bo_f[:], in0=bo_b[:], scalar1=1.0, scalar2=0.0, op0=ALU.mult, op1=ALU.add
+        )
+        scan(2, 0)
+        quant("wo0", 0, 1024)
+        turn("wo1", 0)
+        turn("wo1", 1)
+        scan(2, 1)
+        turn("wo1", 2)
+        turn("wo1", 3)
+        first(3, 0)
+        first(3, 1)
+        scan(2, 2)
+        turn("in2", 0)
+        turn("in2", 1)
+        scan(2, 3)
+        quant("wo1", 0, 1024)
+        quant_x(1, 0, 512)
+        turn("in2", 2)
+        turn("in2", 3)
+        first(3, 2)
+        first(3, 3)
+        weave(2, 0, 256, "pool")
+        weave(2, 256, 256, "pool")
+        S2 = {3: [(0, 0), (0, 1)], 4: [(0, 2), (0, 3)], 5: [(1, 0), (1, 1)], 6: [(1, 2), (1, 3)], 7: [(2, 0), (2, 1)]}
+        for s in range(3, 8):
+            A = {4: "in3"}.get(s)
+            rows = S2.get(s, [])
+            scan(s, 0)
+            if s == 3:
+                quant("in2", 0, 1024)
+            if A:
+                turn(A, 0)
+                turn(A, 1)
+            second(*rows[0], 0, False)
+            second(*rows[0], 1, s >= 5)
+            scan(s, 1)
+            if A:
+                turn(A, 2)
+                turn(A, 3)
+            if s < 7:
+                first(s + 1, 0)
+                first(s + 1, 1)
+            scan(s, 2)
+            second(*rows[1], 0, False)
+            second(*rows[1], 1, True)
+            scan(s, 3)
+            if A:
+                quant(A, 0, 1024)
+            if s < 7:
+                first(s + 1, 2)
+                first(s + 1, 3)
+            quant_x(s - 1, 0, 512)
+            if s < 7:
+                weave(s, 0, 256, "pool")
+                weave(s, 256, 256, "pool")
+        weave(7, 0, 256, "vector")
+        weave(7, 256, 256, "scalar")
+        second(2, 2, 0, False)
+        second(2, 2, 1, True)
+        quant_x(7, 0, 256)
+        second(2, 3, 0, False)
+        second(2, 3, 1, True)
+        quant_x(7, 256, 256)
+        for i in range(4):
+            for h in range(2):
+                second(3, i, h, h == 1 or i >= 1)

@@ -33,13 +33,13 @@ def tile_slru_kernel(tc, inputs, Wi, bi, Wo, bo, params_log, out):
         rawp = ctx.enter_context(tc.tile_pool(name="raw", bufs=1))
         keep = ctx.enter_context(tc.tile_pool(name="keep", bufs=1))
         stg = ctx.enter_context(tc.tile_pool(name="stg", bufs=2))
-        vpool = ctx.enter_context(tc.tile_pool(name="vp", bufs=6))
-        xpool = ctx.enter_context(tc.tile_pool(name="xp", bufs=3))
+        vpool = ctx.enter_context(tc.tile_pool(name="vp", bufs=8))
+        xpool = ctx.enter_context(tc.tile_pool(name="xp", bufs=4))
         gpool = ctx.enter_context(tc.tile_pool(name="gp", bufs=2))
-        opool = ctx.enter_context(tc.tile_pool(name="op", bufs=6))
-        ps_t = ctx.enter_context(tc.psum_pool(name="pst", bufs=3))
+        opool = ctx.enter_context(tc.tile_pool(name="op", bufs=5))
+        ps_t = ctx.enter_context(tc.psum_pool(name="pst", bufs=2))
         ps_1 = ctx.enter_context(tc.psum_pool(name="ps1", bufs=2))
-        ps_2 = ctx.enter_context(tc.psum_pool(name="ps2", bufs=2))
+        ps_2 = ctx.enter_context(tc.psum_pool(name="ps2", bufs=3))
         ps_c = ctx.enter_context(tc.psum_pool(name="psc", bufs=1))
         ctx.enter_context(tc.manual_schedule())
 
@@ -93,7 +93,6 @@ def tile_slru_kernel(tc, inputs, Wi, bi, Wo, bo, params_log, out):
         lam = const.tile([P, 8], F32, name="lam")
         gam = const.tile([P, 8], F32, name="gam")
         gb = const.tile([P, 8], F32, name="gb")
-        bi_f = const.tile([P, 8], F32, name="bi_f")
         lam_p = ps_c.tile([P, 8], F32, name="lam_p")
         bo_f = const.tile([P, H], F32, name="bo_f")
 
@@ -101,8 +100,7 @@ def tile_slru_kernel(tc, inputs, Wi, bi, Wo, bo, params_log, out):
             nc.scalar.activation(out=nu[:], in_=pl[0][:], func=ACTF.Exp)
             nc.scalar.activation(out=lam[:], in_=nu[:], func=ACTF.Exp, scale=-1.0)
             nc.scalar.activation(out=gam[:], in_=pl[1][:], func=ACTF.Exp)
-            nc.vector.tensor_copy(out=bi_f[:], in_=bi_b[:])
-            nc.vector.tensor_tensor(out=gb[:], in0=gam[:], in1=bi_f[:], op=ALU.mult)
+            nc.gpsimd.tensor_tensor(out=gb[:], in0=gam[:], in1=bi_b[:], op=ALU.mult)
 
         codes, scales = {}, {}
         for nm in raw:
@@ -179,17 +177,20 @@ def tile_slru_kernel(tc, inputs, Wi, bi, Wo, bo, params_log, out):
             )
             vs[u, j] = v
 
-        def scan(u, j):
+        def scan(u, j, lo=0, n=CH):
             c, g2 = u // 2, u % 2
             ct = 4 * g2 + j
-            if j == 0:
+            if j == 0 and lo == 0:
                 t = xpool.tile([P, 4, CH], F32, name="xs")
                 xs[u] = t
-            init = 0.0 if (c * CH) % SEQ == 0 else xs[u - 2][:, j, CH - 1 : CH]
+            if lo > 0:
+                init = xs[u][:, j, lo - 1 : lo]
+            else:
+                init = 0.0 if (c * CH) % SEQ == 0 else xs[u - 2][:, j, CH - 1 : CH]
             nc.vector.tensor_tensor_scan(
-                out=xs[u][:, j, :],
-                data0=lam_p[:, ct : ct + 1].to_broadcast([P, CH]),
-                data1=vs[u, j][:],
+                out=xs[u][:, j, lo : lo + n],
+                data0=lam_p[:, ct : ct + 1].to_broadcast([P, n]),
+                data1=vs[u, j][:, lo : lo + n],
                 initial=init,
                 op0=ALU.mult,
                 op1=ALU.add,
@@ -218,13 +219,9 @@ def tile_slru_kernel(tc, inputs, Wi, bi, Wo, bo, params_log, out):
                 in_=gx[u][:, lo : lo + n, :].rearrange("p t j -> p (t j)"),
             )
 
-        outs = {}
+        outs, acc2 = {}, {}
 
-        def second(c, i, h, on_vector):
-            if h == 0:
-                o = opool.tile([P, H], F32, name="o")
-                outs[c, i] = o
-            o = outs[c, i]
+        def second(c, i, h):
             acc = ps_2.tile([P, 512], F32, name="acc2")
             ts = slice(P * i, P * (i + 1))
             wo = "wo%d" % h
@@ -239,6 +236,13 @@ def tile_slru_kernel(tc, inputs, Wi, bi, Wo, bo, params_log, out):
                     start=(g == 0),
                     stop=(g == 1),
                 )
+            acc2[c, i, h] = acc
+
+        def drain(c, i, h, on_vector):
+            if h == 0:
+                o = opool.tile([P, H], F32, name="o")
+                outs[c, i] = o
+            o, acc = outs[c, i], acc2[c, i, h]
             hs = slice(512 * h, 512 * (h + 1))
             if on_vector:
                 nc.vector.tensor_tensor(out=o[:, hs], in0=acc[:], in1=bo_f[:, hs], op=ALU.add)
@@ -253,7 +257,7 @@ def tile_slru_kernel(tc, inputs, Wi, bi, Wo, bo, params_log, out):
 
         for i in range(4):
             turn("in0", i, on_vector=(i % 2 == 1))
-            if i == 1:
+            if i == 0:
                 constants()
             if i % 2 == 1:
                 for g in range(2):
@@ -263,114 +267,200 @@ def tile_slru_kernel(tc, inputs, Wi, bi, Wo, bo, params_log, out):
         turn("wi0", 1, on_vector=True)
         quant("wi0", 0, 256)
         turn("wi0", 2)
-        first(0, 0)
         quant("wi0", 256, 256)
         turn("wi0", 3, on_vector=True)
+        first(0, 0)
         first(0, 1)
         quant("wi0", 512, 256)
+        quant("wi0", 768, 256)
         turn("wi1", 0)
         first(0, 2)
         scan(0, 0)
-        quant("wi0", 768, 256)
         turn("wi1", 1, on_vector=True)
         first(0, 3)
         scan(0, 1)
         turn("wi1", 2)
-        quant("wi1", 0, 512)
         turn("wi1", 3)
-        first(1, 0)
         scan(0, 2)
-        quant("wi1", 512, 512)
-        first(1, 1)
+        quant("wi1", 0, 512)
         turn("in1", 0)
         turn("in1", 1)
+        first(1, 0)
+        first(1, 1)
         scan(0, 3)
+        quant("wi1", 512, 512)
         weave(0, 0, 256, "pool")
-        weave(0, 256, 256, "pool")
-        first(1, 2)
-        turn("in1", 2)
-        turn("in1", 3)
-        first(1, 3)
         scan(1, 0)
+        turn("in1", 2)
+        first(1, 2)
+        turn("in1", 3)
+        weave(0, 256, 256, "scalar")
         scan(1, 1)
-        quant("in1", 0, 1024)
-        first(2, 0)
-        first(2, 1)
+        first(1, 3)
+        scan(1, 2)
+        quant_x(0, 0, 512)
         turn("wo0", 0)
         turn("wo0", 1)
-        scan(1, 2)
-        first(2, 2)
-        first(2, 3)
-        turn("wo0", 2)
-        turn("wo0", 3)
+        quant("in1", 0, 1024)
         scan(1, 3)
-        quant_x(0, 0, 512)
+        turn("wo0", 2)
+        first(2, 0)
+        first(2, 1)
+        turn("wo0", 3)
         weave(1, 0, 256, "pool")
-        weave(1, 256, 256, "pool")
         nc.gpsimd.tensor_scalar(
             out=bo_f[:], in0=bo_b[:], scalar1=1.0, scalar2=0.0, op0=ALU.mult, op1=ALU.add
         )
         scan(2, 0)
+        weave(1, 256, 256, "scalar")
+        first(2, 2)
+        first(2, 3)
+        scan(2, 1)
         quant("wo0", 0, 1024)
         turn("wo1", 0)
         turn("wo1", 1)
-        scan(2, 1)
         turn("wo1", 2)
         turn("wo1", 3)
         first(3, 0)
         first(3, 1)
         scan(2, 2)
+        quant_x(1, 0, 512)
+        scan(2, 3)
         turn("in2", 0)
         turn("in2", 1)
-        scan(2, 3)
+        weave(2, 0, 256, "pool")
+        scan(3, 0)
         quant("wo1", 0, 1024)
-        quant_x(1, 0, 512)
         turn("in2", 2)
-        turn("in2", 3)
         first(3, 2)
         first(3, 3)
-        weave(2, 0, 256, "pool")
-        weave(2, 256, 256, "pool")
-        S2 = {3: [(0, 0), (0, 1)], 4: [(0, 2), (0, 3)], 5: [(1, 0), (1, 1)], 6: [(1, 2), (1, 3)], 7: [(2, 0), (2, 1)]}
-        for s in range(3, 8):
-            A = {4: "in3"}.get(s)
-            rows = S2.get(s, [])
-            scan(s, 0)
-            if s == 3:
-                quant("in2", 0, 1024)
-            if A:
-                turn(A, 0)
-                turn(A, 1)
-            second(*rows[0], 0, False)
-            second(*rows[0], 1, s >= 5)
-            scan(s, 1)
-            if A:
-                turn(A, 2)
-                turn(A, 3)
-            if s < 7:
-                first(s + 1, 0)
-                first(s + 1, 1)
-            scan(s, 2)
-            second(*rows[1], 0, False)
-            second(*rows[1], 1, True)
-            scan(s, 3)
-            if A:
-                quant(A, 0, 1024)
-            if s < 7:
-                first(s + 1, 2)
-                first(s + 1, 3)
-            quant_x(s - 1, 0, 512)
-            if s < 7:
-                weave(s, 0, 256, "pool")
-                weave(s, 256, 256, "pool")
-        weave(7, 0, 256, "vector")
-        weave(7, 256, 256, "scalar")
-        second(2, 2, 0, False)
-        second(2, 2, 1, True)
+        turn("in2", 3)
+        weave(2, 256, 256, "scalar")
+        scan(3, 1)
+        second(0, 0, 0)
+        second(0, 0, 1)
+        drain(0, 0, 0, False)
+        scan(3, 2)
+        drain(0, 0, 1, False)
+        quant("in2", 0, 1024)
+        second(0, 1, 0)
+        first(4, 0)
+        first(4, 1)
+        scan(3, 3)
+        drain(0, 1, 0, True)
+        second(0, 1, 1)
+        quant_x(2, 0, 512)
+        drain(0, 1, 1, False)
+        weave(3, 0, 256, "pool")
+        scan(4, 0)
+        first(4, 2)
+        first(4, 3)
+        turn("in3", 0)
+        turn("in3", 1)
+        weave(3, 256, 256, "scalar")
+        scan(4, 1)
+        second(0, 2, 0)
+        second(0, 2, 1)
+        drain(0, 2, 0, False)
+        scan(4, 2)
+        drain(0, 2, 1, True)
+        first(5, 0)
+        first(5, 1)
+        turn("in3", 2)
+        turn("in3", 3)
+        second(0, 3, 0)
+        second(0, 3, 1)
+        scan(4, 3)
+        quant_x(3, 0, 512)
+        drain(0, 3, 0, False)
+        drain(0, 3, 1, True)
+        first(5, 2)
+        first(5, 3)
+        weave(4, 0, 256, "pool")
+        second(1, 0, 0)
+        second(1, 0, 1)
+        scan(5, 0)
+        quant("in3", 0, 1024)
+        drain(1, 0, 0, False)
+        drain(1, 0, 1, True)
+        weave(4, 256, 256, "scalar")
+        second(1, 1, 0)
+        second(1, 1, 1)
+        scan(5, 1)
+        drain(1, 1, 0, False)
+        first(6, 0)
+        first(6, 1)
+        scan(5, 2)
+        drain(1, 1, 1, True)
+        second(1, 2, 0)
+        second(1, 2, 1)
+        first(6, 2)
+        first(6, 3)
+        quant_x(4, 0, 512)
+        drain(1, 2, 0, False)
+        scan(5, 3)
+        drain(1, 2, 1, True)
+        weave(5, 0, 256, "pool")
+        second(1, 3, 0)
+        second(1, 3, 1)
+        scan(6, 0, 0, 256)
+        first(7, 0)
+        drain(1, 3, 0, False)
+        weave(5, 256, 256, "scalar")
+        scan(6, 1, 0, 256)
+        drain(1, 3, 1, True)
+        first(7, 1)
+        scan(6, 2, 0, 256)
+        first(7, 2)
+        first(7, 3)
+        scan(6, 3, 0, 256)
+        quant_x(5, 0, 512)
+        second(2, 0, 0)
+        second(2, 0, 1)
+        weave(6, 0, 256, "scalar")
+        drain(2, 0, 0, False)
+        scan(7, 0, 0, 256)
+        scan(7, 1, 0, 256)
+        drain(2, 0, 1, True)
+        second(2, 1, 0)
+        second(2, 1, 1)
+        scan(7, 2, 0, 256)
+        drain(2, 1, 0, False)
+        scan(7, 3, 0, 256)
+        drain(2, 1, 1, True)
+        second(2, 2, 0)
+        second(2, 2, 1)
+        quant_x(6, 0, 256)
+        weave(7, 0, 256, "scalar")
+        scan(6, 0, 256, 256)
+        drain(2, 2, 0, False)
+        scan(6, 1, 256, 256)
+        drain(2, 2, 1, True)
+        second(2, 3, 0)
+        second(2, 3, 1)
+        scan(6, 2, 256, 256)
+        drain(2, 3, 0, False)
+        scan(6, 3, 256, 256)
         quant_x(7, 0, 256)
-        second(2, 3, 0, False)
-        second(2, 3, 1, True)
+        drain(2, 3, 1, True)
+        second(3, 0, 0)
+        second(3, 0, 1)
+        weave(6, 256, 256, "scalar")
+        scan(7, 0, 256, 256)
+        drain(3, 0, 0, False)
+        scan(7, 1, 256, 256)
+        drain(3, 0, 1, True)
+        second(3, 1, 0)
+        second(3, 1, 1)
+        scan(7, 2, 256, 256)
+        quant_x(6, 256, 256)
+        scan(7, 3, 256, 256)
+        drain(3, 1, 0, True)
+        weave(7, 256, 128, "vector")
+        weave(7, 384, 128, "scalar")
+        drain(3, 1, 1, True)
         quant_x(7, 256, 256)
-        for i in range(4):
+        for i in range(2, 4):
             for h in range(2):
-                second(3, i, h, h == 1 or i >= 1)
+                second(3, i, h)
+                drain(3, i, h, (i, h) != (2, 1))

@@ -37,9 +37,7 @@ def tile_slru_kernel(tc, inputs, Wi, bi, Wo, bo, params_log, out):
         xpool = ctx.enter_context(tc.tile_pool(name="xp", bufs=4))
         gpool = ctx.enter_context(tc.tile_pool(name="gp", bufs=2))
         opool = ctx.enter_context(tc.tile_pool(name="op", bufs=5))
-        ps_t = ctx.enter_context(tc.psum_pool(name="pst", bufs=2))
-        ps_1 = ctx.enter_context(tc.psum_pool(name="ps1", bufs=2))
-        ps_2 = ctx.enter_context(tc.psum_pool(name="ps2", bufs=3))
+        psum = ctx.enter_context(tc.psum_pool(name="ps", bufs=7))
         ps_c = ctx.enter_context(tc.psum_pool(name="psc", bufs=1))
         ctx.enter_context(tc.manual_schedule())
 
@@ -120,7 +118,7 @@ def tile_slru_kernel(tc, inputs, Wi, bi, Wo, bo, params_log, out):
             if i == 0:
                 stage = stg.tile([P, 2048], F32, name="stage", align_bytes=64)
                 stages[nm] = stage
-            bank = ps_t.tile([P, 2, 2, P], F32, name="bank")
+            bank = psum.tile([P, 2, 2, P], F32, name="bank", tag="bank")
             words = raw[nm][:, i, :].bitcast(F32)
             for g in range(2):
                 for u in range(2):
@@ -153,7 +151,7 @@ def tile_slru_kernel(tc, inputs, Wi, bi, Wo, bo, params_log, out):
         def first(u, j):
             c, g2 = u // 2, u % 2
             ct = 4 * g2 + j
-            acc = ps_1.tile([P, CH], F32, name="acc1")
+            acc = psum.tile([P, CH], F32, name="acc1", tag="bank")
             wi, xi = "wi%d" % g2, "in%d" % c
             for g in range(2):
                 w = slice(256 * j + 128 * g, 256 * j + 128 * (g + 1))
@@ -222,7 +220,7 @@ def tile_slru_kernel(tc, inputs, Wi, bi, Wo, bo, params_log, out):
         outs, acc2 = {}, {}
 
         def second(c, i, h):
-            acc = ps_2.tile([P, 512], F32, name="acc2")
+            acc = psum.tile([P, 512], F32, name="acc2", tag="bank")
             ts = slice(P * i, P * (i + 1))
             wo = "wo%d" % h
             for g in range(2):
@@ -263,204 +261,203 @@ def tile_slru_kernel(tc, inputs, Wi, bi, Wo, bo, params_log, out):
                 for g in range(2):
                     quant("in0", 512 * g + 128 * (i - 1), 256)
         nc.tensor.matmul(out=lam_p[:], lhsT=ident[:], rhs=lam[:], start=True, stop=True)
-        turn("wi0", 0)
-        turn("wi0", 1, on_vector=True)
-        quant("wi0", 0, 256)
-        turn("wi0", 2)
-        quant("wi0", 256, 256)
-        turn("wi0", 3, on_vector=True)
+        for j in range(4):
+            turn("wi0", j, on_vector=(j % 2 == 1))
+            if j % 2 == 1:
+                quant("wi0", 256 * (j - 1), 256)
+                quant("wi0", 256 * j, 256)
+        turn("wi1", 0)
         first(0, 0)
         first(0, 1)
-        quant("wi0", 512, 256)
-        quant("wi0", 768, 256)
-        turn("wi1", 0)
-        first(0, 2)
         scan(0, 0)
         turn("wi1", 1, on_vector=True)
+        first(0, 2)
         first(0, 3)
+        quant("wi1", 0, 512)
         scan(0, 1)
         turn("wi1", 2)
-        turn("wi1", 3)
+        turn("wi1", 3, on_vector=True)
         scan(0, 2)
-        quant("wi1", 0, 512)
-        turn("in1", 0)
-        turn("in1", 1)
         first(1, 0)
         first(1, 1)
-        scan(0, 3)
         quant("wi1", 512, 512)
-        weave(0, 0, 256, "pool")
-        scan(1, 0)
+        turn("in1", 0)
+        turn("in1", 1)
+        scan(0, 3)
         turn("in1", 2)
-        first(1, 2)
         turn("in1", 3)
-        weave(0, 256, 256, "scalar")
-        scan(1, 1)
+        first(1, 2)
         first(1, 3)
-        scan(1, 2)
-        quant_x(0, 0, 512)
-        turn("wo0", 0)
-        turn("wo0", 1)
-        quant("in1", 0, 1024)
-        scan(1, 3)
-        turn("wo0", 2)
-        first(2, 0)
-        first(2, 1)
-        turn("wo0", 3)
-        weave(1, 0, 256, "pool")
         nc.gpsimd.tensor_scalar(
             out=bo_f[:], in0=bo_b[:], scalar1=1.0, scalar2=0.0, op0=ALU.mult, op1=ALU.add
         )
-        scan(2, 0)
-        weave(1, 256, 256, "scalar")
+        weave(0, 0, 256, "pool")
+        scan(1, 0)
+        turn("wo0", 0)
+        weave(0, 256, 256, "scalar")
+        scan(1, 1)
+        quant("in1", 0, 1024)
+        turn("wo0", 1)
+        first(2, 0)
+        first(2, 1)
+        scan(1, 2)
+        turn("wo0", 2)
+        turn("wo0", 3)
         first(2, 2)
         first(2, 3)
-        scan(2, 1)
-        quant("wo0", 0, 1024)
-        turn("wo1", 0)
-        turn("wo1", 1)
-        turn("wo1", 2)
-        turn("wo1", 3)
-        first(3, 0)
-        first(3, 1)
-        scan(2, 2)
-        quant_x(1, 0, 512)
-        scan(2, 3)
+        scan(1, 3)
+        quant_x(0, 0, 512)
+        weave(1, 0, 256, "pool")
+        scan(2, 0)
         turn("in2", 0)
         turn("in2", 1)
-        weave(2, 0, 256, "pool")
-        scan(3, 0)
-        quant("wo1", 0, 1024)
+        weave(1, 256, 256, "scalar")
+        scan(2, 1)
+        quant("wo0", 0, 1024)
+        first(3, 0)
+        first(3, 1)
         turn("in2", 2)
+        turn("in2", 3)
+        scan(2, 2)
         first(3, 2)
         first(3, 3)
-        turn("in2", 3)
+        turn("wo1", 0)
+        turn("wo1", 1)
+        scan(2, 3)
+        quant_x(1, 0, 512)
+        turn("wo1", 2)
+        turn("wo1", 3)
+        weave(2, 0, 256, "pool")
+        scan(3, 0)
+        quant("in2", 0, 1024)
         weave(2, 256, 256, "scalar")
         scan(3, 1)
-        second(0, 0, 0)
-        second(0, 0, 1)
-        drain(0, 0, 0, False)
-        scan(3, 2)
-        drain(0, 0, 1, False)
-        quant("in2", 0, 1024)
-        second(0, 1, 0)
         first(4, 0)
         first(4, 1)
-        scan(3, 3)
-        drain(0, 1, 0, True)
-        second(0, 1, 1)
-        quant_x(2, 0, 512)
-        drain(0, 1, 1, False)
-        weave(3, 0, 256, "pool")
-        scan(4, 0)
+        scan(3, 2)
+        quant("wo1", 0, 1024)
         first(4, 2)
         first(4, 3)
+        second(0, 0, 0)
+        second(0, 0, 1)
+        scan(3, 3)
+        drain(0, 0, 0, False)
+        second(0, 1, 0)
+        second(0, 1, 1)
+        quant_x(2, 0, 512)
+        drain(0, 0, 1, False)
+        weave(3, 0, 256, "pool")
         turn("in3", 0)
         turn("in3", 1)
+        scan(4, 0)
+        drain(0, 1, 0, True)
+        drain(0, 1, 1, False)
         weave(3, 256, 256, "scalar")
-        scan(4, 1)
         second(0, 2, 0)
         second(0, 2, 1)
-        drain(0, 2, 0, False)
-        scan(4, 2)
-        drain(0, 2, 1, True)
+        scan(4, 1)
         first(5, 0)
         first(5, 1)
         turn("in3", 2)
         turn("in3", 3)
+        drain(0, 2, 0, False)
+        scan(4, 2)
+        drain(0, 2, 1, True)
         second(0, 3, 0)
         second(0, 3, 1)
+        first(5, 2)
+        first(5, 3)
         scan(4, 3)
         quant_x(3, 0, 512)
         drain(0, 3, 0, False)
-        drain(0, 3, 1, True)
-        first(5, 2)
-        first(5, 3)
         weave(4, 0, 256, "pool")
         second(1, 0, 0)
         second(1, 0, 1)
         scan(5, 0)
         quant("in3", 0, 1024)
+        drain(0, 3, 1, True)
         drain(1, 0, 0, False)
-        drain(1, 0, 1, True)
         weave(4, 256, 256, "scalar")
         second(1, 1, 0)
         second(1, 1, 1)
         scan(5, 1)
-        drain(1, 1, 0, False)
+        drain(1, 0, 1, True)
         first(6, 0)
         first(6, 1)
+        drain(1, 1, 0, False)
         scan(5, 2)
-        drain(1, 1, 1, True)
         second(1, 2, 0)
         second(1, 2, 1)
         first(6, 2)
         first(6, 3)
+        drain(1, 1, 1, True)
+        scan(5, 3)
         quant_x(4, 0, 512)
         drain(1, 2, 0, False)
-        scan(5, 3)
-        drain(1, 2, 1, True)
         weave(5, 0, 256, "pool")
         second(1, 3, 0)
         second(1, 3, 1)
         scan(6, 0, 0, 256)
+        drain(1, 2, 1, True)
         first(7, 0)
-        drain(1, 3, 0, False)
+        first(7, 1)
         weave(5, 256, 256, "scalar")
         scan(6, 1, 0, 256)
-        drain(1, 3, 1, True)
-        first(7, 1)
         scan(6, 2, 0, 256)
+        drain(1, 3, 0, False)
         first(7, 2)
         first(7, 3)
         scan(6, 3, 0, 256)
+        drain(1, 3, 1, True)
+        scan(7, 0, 0, 256)
+        weave(6, 0, 256, "scalar")
+        scan(7, 1, 0, 256)
         quant_x(5, 0, 512)
+        scan(7, 2, 0, 256)
+        scan(7, 3, 0, 256)
         second(2, 0, 0)
         second(2, 0, 1)
-        weave(6, 0, 256, "scalar")
-        drain(2, 0, 0, False)
-        scan(7, 0, 0, 256)
-        scan(7, 1, 0, 256)
-        drain(2, 0, 1, True)
         second(2, 1, 0)
         second(2, 1, 1)
-        scan(7, 2, 0, 256)
-        drain(2, 1, 0, False)
-        scan(7, 3, 0, 256)
-        drain(2, 1, 1, True)
+        scan(6, 0, 256, 256)
+        quant_x(6, 0, 256)
+        drain(2, 0, 0, False)
+        weave(7, 0, 256, "scalar")
+        scan(6, 1, 256, 256)
+        drain(2, 0, 1, True)
         second(2, 2, 0)
         second(2, 2, 1)
-        quant_x(6, 0, 256)
-        weave(7, 0, 256, "scalar")
-        scan(6, 0, 256, 256)
-        drain(2, 2, 0, False)
-        scan(6, 1, 256, 256)
-        drain(2, 2, 1, True)
+        scan(6, 2, 256, 256)
+        drain(2, 1, 0, True)
+        drain(2, 1, 1, True)
+        scan(6, 3, 256, 256)
         second(2, 3, 0)
         second(2, 3, 1)
-        scan(6, 2, 256, 256)
-        drain(2, 3, 0, False)
-        scan(6, 3, 256, 256)
+        drain(2, 2, 0, True)
+        drain(2, 2, 1, True)
         quant_x(7, 0, 256)
-        drain(2, 3, 1, True)
+        scan(7, 0, 256, 256)
+        weave(6, 256, 256, "scalar")
+        drain(2, 3, 0, True)
         second(3, 0, 0)
         second(3, 0, 1)
-        weave(6, 256, 256, "scalar")
-        scan(7, 0, 256, 256)
-        drain(3, 0, 0, False)
         scan(7, 1, 256, 256)
-        drain(3, 0, 1, True)
+        drain(2, 3, 1, True)
         second(3, 1, 0)
         second(3, 1, 1)
         scan(7, 2, 256, 256)
-        quant_x(6, 256, 256)
+        drain(3, 0, 0, True)
         scan(7, 3, 256, 256)
-        drain(3, 1, 0, True)
+        quant_x(6, 256, 256)
         weave(7, 256, 128, "vector")
         weave(7, 384, 128, "scalar")
-        drain(3, 1, 1, True)
+        drain(3, 0, 1, True)
+        drain(3, 1, 0, True)
         quant_x(7, 256, 256)
+        drain(3, 1, 1, True)
         for i in range(2, 4):
             for h in range(2):
                 second(3, i, h)
-                drain(3, i, h, (i, h) != (2, 1))
+        for i in range(2, 4):
+            for h in range(2):
+                drain(3, i, h, True)

@@ -57,10 +57,10 @@ def tile_slru_kernel(tc, inputs, Wi, bi, Wo, bo, params_log, out):
                 return Wi[i * 512 : (i + 1) * 512, :].rearrange("(m e) h -> m e h", e=4)
             return Wo[i * 512 : (i + 1) * 512, :].rearrange("(i p) u -> p i u", p=P)
 
-        def load(nm, pieces):
+        def load(nm, pieces, i0=0, i1=None):
             src = source(nm)
             n = 4 // pieces
-            for i in range(pieces):
+            for i in range(i0, pieces if i1 is None else i1):
                 nc.sync.dma_start(
                     out=raw[nm][:, n * i : n * (i + 1), :], in_=src[:, n * i : n * (i + 1), :]
                 )
@@ -76,8 +76,9 @@ def tile_slru_kernel(tc, inputs, Wi, bi, Wo, bo, params_log, out):
             out=bi_b[:].rearrange("m (a e) -> m a e", e=4),
             in_=bi.rearrange("(a m e) -> m a e", a=2, e=4),
         )
-        load("in0", 4)
+        load("in0", 4, 0, 2)
         load("wi0", 4)
+        load("in0", 4, 2, 4)
         load("wi1", 2)
         load("in1", 2)
         load("wo0", 1)
@@ -146,16 +147,29 @@ def tile_slru_kernel(tc, inputs, Wi, bi, Wo, bo, params_log, out):
                 in_=stages[nm][:, 2 * lo : 2 * (lo + n)].bitcast(BF16),
             )
 
+        def warm(n):
+            scrap = psum.tile([P, 512], F32, name="scrap", tag="bank")
+            for k in range(n):
+                nc.tensor.matmul_mx(
+                    out=scrap[:],
+                    lhsT=codes["in0"][:, 0:P].bitcast(FP8X4),
+                    lhsT_scale=scales["in0"][:, 0:P],
+                    rhs=codes["in0"][:, 0:512].bitcast(FP8X4),
+                    rhs_scale=scales["in0"][:, 0:512],
+                    start=True,
+                    stop=True,
+                )
+
         acc1, vs, xs, gx = {}, {}, {}, {}
 
-        def first(u, j):
+        def first(u, j, lo=0, n=CH):
             c, g2 = u // 2, u % 2
             ct = 4 * g2 + j
-            acc = psum.tile([P, CH], F32, name="acc1", tag="bank")
+            acc = psum.tile([P, n], F32, name="acc1", tag="bank")
             wi, xi = "wi%d" % g2, "in%d" % c
             for g in range(2):
                 w = slice(256 * j + 128 * g, 256 * j + 128 * (g + 1))
-                r = slice(512 * g, 512 * (g + 1))
+                r = slice(512 * g + lo, 512 * g + lo + n)
                 nc.tensor.matmul_mx(
                     out=acc[:],
                     lhsT=codes[wi][:, w].bitcast(FP8X4),
@@ -165,15 +179,16 @@ def tile_slru_kernel(tc, inputs, Wi, bi, Wo, bo, params_log, out):
                     start=(g == 0),
                     stop=(g == 1),
                 )
-            v = vpool.tile([P, CH], F32, name="v")
+            if lo == 0:
+                v = vpool.tile([P, CH], F32, name="v")
+                vs[u, j] = v
             nc.scalar.activation(
-                out=v[:],
+                out=vs[u, j][:, lo : lo + n],
                 in_=acc[:],
                 func=ACTF.Identity,
                 scale=gam[:, ct : ct + 1],
                 bias=gb[:, ct : ct + 1],
             )
-            vs[u, j] = v
 
         def scan(u, j, lo=0, n=CH):
             c, g2 = u // 2, u % 2
@@ -253,39 +268,53 @@ def tile_slru_kernel(tc, inputs, Wi, bi, Wo, bo, params_log, out):
             elif h == 1:
                 nc.sync.dma_start(out=o_out[r0 : r0 + P, :], in_=o[:])
 
-        for i in range(4):
-            turn("in0", i, on_vector=(i % 2 == 1))
-            if i == 0:
-                constants()
-            if i % 2 == 1:
-                for g in range(2):
-                    quant("in0", 512 * g + 128 * (i - 1), 256)
+        turn("in0", 0)
+        constants()
+        turn("in0", 1, on_vector=True)
+        for g in range(2):
+            quant("in0", 512 * g, 256)
+        turn("wi0", 0)
+        turn("wi0", 1, on_vector=True)
+        quant("wi0", 0, 256)
+        turn("wi0", 2)
+        quant("wi0", 256, 256)
+        turn("wi0", 3, on_vector=True)
         nc.tensor.matmul(out=lam_p[:], lhsT=ident[:], rhs=lam[:], start=True, stop=True)
-        for j in range(4):
-            turn("wi0", j, on_vector=(j % 2 == 1))
-            if j % 2 == 1:
-                quant("wi0", 256 * (j - 1), 256)
-                quant("wi0", 256 * j, 256)
+        first(0, 0, 0, 256)
+        turn("in0", 2)
+        first(0, 1, 0, 256)
+        quant("wi0", 512, 256)
+        quant("wi0", 768, 256)
+        scan(0, 0, 0, 256)
+        turn("in0", 3, on_vector=True)
+        first(0, 2, 0, 256)
+        first(0, 3, 0, 256)
+        scan(0, 1, 0, 256)
+        for g in range(2):
+            quant("in0", 512 * g + 256, 256)
         turn("wi1", 0)
-        first(0, 0)
-        first(0, 1)
-        scan(0, 0)
+        scan(0, 2, 0, 256)
         turn("wi1", 1, on_vector=True)
-        first(0, 2)
-        first(0, 3)
+        first(0, 0, 256, 256)
+        first(0, 1, 256, 256)
+        scan(0, 3, 0, 256)
         quant("wi1", 0, 512)
-        scan(0, 1)
         turn("wi1", 2)
+        scan(0, 0, 256, 256)
+        first(0, 2, 256, 256)
+        first(0, 3, 256, 256)
+        scan(0, 1, 256, 256)
         turn("wi1", 3, on_vector=True)
-        scan(0, 2)
+        scan(0, 2, 256, 256)
+        turn("in1", 0)
+        turn("in1", 1)
         first(1, 0)
         first(1, 1)
         quant("wi1", 512, 512)
-        turn("in1", 0)
-        turn("in1", 1)
-        scan(0, 3)
+        scan(0, 3, 256, 256)
         turn("in1", 2)
         turn("in1", 3)
+        warm(2)
         first(1, 2)
         first(1, 3)
         nc.gpsimd.tensor_scalar(
@@ -298,6 +327,7 @@ def tile_slru_kernel(tc, inputs, Wi, bi, Wo, bo, params_log, out):
         scan(1, 1)
         quant("in1", 0, 1024)
         turn("wo0", 1)
+        warm(2)
         first(2, 0)
         first(2, 1)
         scan(1, 2)
@@ -328,117 +358,92 @@ def tile_slru_kernel(tc, inputs, Wi, bi, Wo, bo, params_log, out):
         turn("wo1", 2)
         turn("wo1", 3)
         weave(2, 0, 256, "pool")
-        scan(3, 0)
-        quant("in2", 0, 1024)
-        weave(2, 256, 256, "scalar")
-        scan(3, 1)
-        first(4, 0)
-        first(4, 1)
-        scan(3, 2)
-        quant("wo1", 0, 1024)
-        first(4, 2)
-        first(4, 3)
-        second(0, 0, 0)
-        second(0, 0, 1)
-        scan(3, 3)
-        drain(0, 0, 0, False)
-        second(0, 1, 0)
-        second(0, 1, 1)
-        quant_x(2, 0, 512)
-        drain(0, 0, 1, False)
-        weave(3, 0, 256, "pool")
-        turn("in3", 0)
-        turn("in3", 1)
-        scan(4, 0)
-        drain(0, 1, 0, True)
-        drain(0, 1, 1, False)
-        weave(3, 256, 256, "scalar")
-        second(0, 2, 0)
-        second(0, 2, 1)
-        scan(4, 1)
-        first(5, 0)
-        first(5, 1)
-        turn("in3", 2)
-        turn("in3", 3)
-        drain(0, 2, 0, False)
-        scan(4, 2)
-        drain(0, 2, 1, True)
-        second(0, 3, 0)
-        second(0, 3, 1)
-        first(5, 2)
-        first(5, 3)
-        scan(4, 3)
-        quant_x(3, 0, 512)
-        drain(0, 3, 0, False)
-        weave(4, 0, 256, "pool")
-        second(1, 0, 0)
-        second(1, 0, 1)
-        scan(5, 0)
-        quant("in3", 0, 1024)
-        drain(0, 3, 1, True)
-        drain(1, 0, 0, False)
-        weave(4, 256, 256, "scalar")
-        second(1, 1, 0)
-        second(1, 1, 1)
-        scan(5, 1)
-        drain(1, 0, 1, True)
-        first(6, 0)
-        first(6, 1)
-        drain(1, 1, 0, False)
-        scan(5, 2)
-        second(1, 2, 0)
-        second(1, 2, 1)
-        first(6, 2)
-        first(6, 3)
-        drain(1, 1, 1, True)
-        scan(5, 3)
-        quant_x(4, 0, 512)
-        drain(1, 2, 0, False)
-        weave(5, 0, 256, "pool")
-        second(1, 3, 0)
-        second(1, 3, 1)
+        rows = [(c, i) for c in range(NCH) for i in range(4)]
+        late = []
+        for s in range(3, 6):
+            ra, rb = rows[2 * s - 6], rows[2 * s - 5]
+            scan(s, 0)
+            if s == 3:
+                quant("in2", 0, 1024)
+            if s == 5:
+                quant("in3", 0, 1024)
+            if s > 3:
+                drain(*late[0], 0, False)
+                drain(*late[0], 1, True)
+            weave(s - 1, 256, 256, "scalar")
+            first(s + 1, 0)
+            first(s + 1, 1)
+            scan(s, 1)
+            if s == 3:
+                quant("wo1", 0, 1024)
+            second(*ra, 0)
+            second(*ra, 1)
+            if s == 4:
+                turn("in3", 0)
+                turn("in3", 1)
+                turn("in3", 2)
+                turn("in3", 3)
+            first(s + 1, 2)
+            first(s + 1, 3)
+            scan(s, 2)
+            drain(*ra, 0, False)
+            drain(*ra, 1, True)
+            second(*rb, 0)
+            second(*rb, 1)
+            late = [rb]
+            scan(s, 3)
+            quant_x(s - 1, 0, 512)
+            weave(s, 0, 256, "pool")
         scan(6, 0, 0, 256)
-        drain(1, 2, 1, True)
+        drain(1, 1, 0, False)
+        drain(1, 1, 1, True)
         first(7, 0)
         first(7, 1)
         weave(5, 256, 256, "scalar")
         scan(6, 1, 0, 256)
+        second(1, 2, 0)
+        second(1, 2, 1)
         scan(6, 2, 0, 256)
-        drain(1, 3, 0, False)
         first(7, 2)
         first(7, 3)
         scan(6, 3, 0, 256)
-        drain(1, 3, 1, True)
+        drain(1, 2, 0, False)
+        drain(1, 2, 1, True)
+        second(1, 3, 0)
+        second(1, 3, 1)
         scan(7, 0, 0, 256)
         weave(6, 0, 256, "scalar")
         scan(7, 1, 0, 256)
         quant_x(5, 0, 512)
-        scan(7, 2, 0, 256)
-        scan(7, 3, 0, 256)
         second(2, 0, 0)
         second(2, 0, 1)
+        scan(7, 2, 0, 256)
+        drain(1, 3, 0, False)
+        drain(1, 3, 1, False)
+        scan(7, 3, 0, 256)
         second(2, 1, 0)
         second(2, 1, 1)
+        weave(7, 0, 256, "scalar")
         scan(6, 0, 256, 256)
         quant_x(6, 0, 256)
         drain(2, 0, 0, False)
-        weave(7, 0, 256, "scalar")
-        scan(6, 1, 256, 256)
         drain(2, 0, 1, True)
+        scan(6, 1, 256, 256)
         second(2, 2, 0)
         second(2, 2, 1)
-        scan(6, 2, 256, 256)
-        drain(2, 1, 0, True)
+        drain(2, 1, 0, False)
         drain(2, 1, 1, True)
-        scan(6, 3, 256, 256)
+        scan(6, 2, 256, 256)
         second(2, 3, 0)
         second(2, 3, 1)
-        drain(2, 2, 0, True)
+        scan(6, 3, 256, 256)
+        drain(2, 2, 0, False)
         drain(2, 2, 1, True)
         quant_x(7, 0, 256)
         scan(7, 0, 256, 256)
         weave(6, 256, 256, "scalar")
-        drain(2, 3, 0, True)
+        drain(2, 3, 0, False)
+        warm(4)
         second(3, 0, 0)
         second(3, 0, 1)
         scan(7, 1, 256, 256)
@@ -455,6 +460,7 @@ def tile_slru_kernel(tc, inputs, Wi, bi, Wo, bo, params_log, out):
         drain(3, 1, 0, True)
         quant_x(7, 256, 256)
         drain(3, 1, 1, True)
+        warm(6)
         for i in range(2, 4):
             for h in range(2):
                 second(3, i, h)

@@ -147,19 +147,6 @@ def tile_slru_kernel(tc, inputs, Wi, bi, Wo, bo, params_log, out):
                 in_=stages[nm][:, 2 * lo : 2 * (lo + n)].bitcast(BF16),
             )
 
-        def warm(n):
-            scrap = psum.tile([P, 512], F32, name="scrap", tag="bank")
-            for k in range(n):
-                nc.tensor.matmul_mx(
-                    out=scrap[:],
-                    lhsT=codes["in0"][:, 0:P].bitcast(FP8X4),
-                    lhsT_scale=scales["in0"][:, 0:P],
-                    rhs=codes["in0"][:, 0:512].bitcast(FP8X4),
-                    rhs_scale=scales["in0"][:, 0:512],
-                    start=True,
-                    stop=True,
-                )
-
         acc1, vs, xs, gx = {}, {}, {}, {}
 
         def first(u, j, lo=0, n=CH):
@@ -314,20 +301,18 @@ def tile_slru_kernel(tc, inputs, Wi, bi, Wo, bo, params_log, out):
         scan(0, 3, 256, 256)
         turn("in1", 2)
         turn("in1", 3)
-        warm(2)
         first(1, 2)
         first(1, 3)
         nc.gpsimd.tensor_scalar(
             out=bo_f[:], in0=bo_b[:], scalar1=1.0, scalar2=0.0, op0=ALU.mult, op1=ALU.add
         )
-        weave(0, 0, 256, "pool")
+        weave(0, 0, 256, "vector")
         scan(1, 0)
         turn("wo0", 0)
         weave(0, 256, 256, "scalar")
         scan(1, 1)
         quant("in1", 0, 1024)
         turn("wo0", 1)
-        warm(2)
         first(2, 0)
         first(2, 1)
         scan(1, 2)
@@ -337,7 +322,7 @@ def tile_slru_kernel(tc, inputs, Wi, bi, Wo, bo, params_log, out):
         first(2, 3)
         scan(1, 3)
         quant_x(0, 0, 512)
-        weave(1, 0, 256, "pool")
+        weave(1, 0, 256, "vector")
         scan(2, 0)
         turn("in2", 0)
         turn("in2", 1)
@@ -357,7 +342,7 @@ def tile_slru_kernel(tc, inputs, Wi, bi, Wo, bo, params_log, out):
         quant_x(1, 0, 512)
         turn("wo1", 2)
         turn("wo1", 3)
-        weave(2, 0, 256, "pool")
+        weave(2, 0, 256, "vector")
         rows = [(c, i) for c in range(NCH) for i in range(4)]
         late = []
         for s in range(3, 6):
@@ -443,7 +428,6 @@ def tile_slru_kernel(tc, inputs, Wi, bi, Wo, bo, params_log, out):
         scan(7, 0, 256, 256)
         weave(6, 256, 256, "scalar")
         drain(2, 3, 0, False)
-        warm(4)
         second(3, 0, 0)
         second(3, 0, 1)
         scan(7, 1, 256, 256)
@@ -453,17 +437,18 @@ def tile_slru_kernel(tc, inputs, Wi, bi, Wo, bo, params_log, out):
         scan(7, 2, 256, 256)
         drain(3, 0, 0, True)
         scan(7, 3, 256, 256)
-        quant_x(6, 256, 256)
         weave(7, 256, 128, "vector")
         weave(7, 384, 128, "scalar")
+        quant_x(6, 256, 256)
+        quant_x(7, 256, 128)
         drain(3, 0, 1, True)
+        second(3, 2, 0)
+        second(3, 2, 1)
+        quant_x(7, 384, 128)
         drain(3, 1, 0, True)
-        quant_x(7, 256, 256)
         drain(3, 1, 1, True)
-        warm(6)
-        for i in range(2, 4):
-            for h in range(2):
-                second(3, i, h)
+        second(3, 3, 0)
+        second(3, 3, 1)
         for i in range(2, 4):
             for h in range(2):
                 drain(3, i, h, True)

@@ -67,17 +67,17 @@ def tile_slru_kernel(tc, inputs, Wi, bi, Wo, bo, params_log, out):
 
         pl = [const.tile([P, 8], BF16, name="pl%d" % r) for r in range(2)]
         bi_b = const.tile([P, 8], BF16, name="bi_b")
+        load("in0", 4, 0, 2)
+        load("wi0", 4)
         for r in range(2):
-            nc.scalar.dma_start(
+            nc.sync.dma_start(
                 out=pl[r][:].rearrange("m (a e) -> m a e", e=4),
                 in_=params_log[r].rearrange("(a m e) -> m a e", a=2, e=4),
             )
-        nc.scalar.dma_start(
+        nc.sync.dma_start(
             out=bi_b[:].rearrange("m (a e) -> m a e", e=4),
             in_=bi.rearrange("(a m e) -> m a e", a=2, e=4),
         )
-        load("in0", 4, 0, 2)
-        load("wi0", 4)
         load("in0", 4, 2, 4)
         load("wi1", 2)
         load("in1", 2)
@@ -256,7 +256,6 @@ def tile_slru_kernel(tc, inputs, Wi, bi, Wo, bo, params_log, out):
                 nc.sync.dma_start(out=o_out[r0 : r0 + P, :], in_=o[:])
 
         turn("in0", 0)
-        constants()
         turn("in0", 1, on_vector=True)
         for g in range(2):
             quant("in0", 512 * g, 256)
@@ -266,12 +265,13 @@ def tile_slru_kernel(tc, inputs, Wi, bi, Wo, bo, params_log, out):
         turn("wi0", 2)
         quant("wi0", 256, 256)
         turn("wi0", 3, on_vector=True)
-        nc.tensor.matmul(out=lam_p[:], lhsT=ident[:], rhs=lam[:], start=True, stop=True)
+        constants()
         first(0, 0, 0, 256)
         turn("in0", 2)
         first(0, 1, 0, 256)
         quant("wi0", 512, 256)
         quant("wi0", 768, 256)
+        nc.tensor.matmul(out=lam_p[:], lhsT=ident[:], rhs=lam[:], start=True, stop=True)
         scan(0, 0, 0, 256)
         turn("in0", 3, on_vector=True)
         first(0, 2, 0, 256)

@@ -34,9 +34,9 @@ def tile_slru_kernel(tc, inputs, Wi, bi, Wo, bo, params_log, out):
         keep = ctx.enter_context(tc.tile_pool(name="keep", bufs=1))
         stg = ctx.enter_context(tc.tile_pool(name="stg", bufs=2))
         vpool = ctx.enter_context(tc.tile_pool(name="vp", bufs=8))
-        xpool = ctx.enter_context(tc.tile_pool(name="xp", bufs=4))
+        xpool = ctx.enter_context(tc.tile_pool(name="xp", bufs=3))
         gpool = ctx.enter_context(tc.tile_pool(name="gp", bufs=2))
-        opool = ctx.enter_context(tc.tile_pool(name="op", bufs=5))
+        opool = ctx.enter_context(tc.tile_pool(name="op", bufs=7))
         psum = ctx.enter_context(tc.psum_pool(name="ps", bufs=7))
         ps_c = ctx.enter_context(tc.psum_pool(name="psc", bufs=1))
         ctx.enter_context(tc.manual_schedule())
@@ -250,7 +250,7 @@ def tile_slru_kernel(tc, inputs, Wi, bi, Wo, bo, params_log, out):
                 nc.scalar.copy(out=o[:, hs], in_=acc[:])
                 nc.gpsimd.tensor_tensor(out=o[:, hs], in0=o[:, hs], in1=bo_f[:, hs], op=ALU.add)
             r0 = c * CH + i * P
-            if c == 3 and i == 3:
+            if c == NCH - 1 and i >= 2:
                 nc.sync.dma_start(out=o_out[r0 : r0 + P, hs], in_=o[:, hs])
             elif h == 1:
                 nc.sync.dma_start(out=o_out[r0 : r0 + P, :], in_=o[:])
@@ -263,9 +263,9 @@ def tile_slru_kernel(tc, inputs, Wi, bi, Wo, bo, params_log, out):
         turn("wi0", 1, on_vector=True)
         quant("wi0", 0, 256)
         turn("wi0", 2)
+        constants()
         quant("wi0", 256, 256)
         turn("wi0", 3, on_vector=True)
-        constants()
         first(0, 0, 0, 256)
         turn("in0", 2)
         first(0, 1, 0, 256)
@@ -291,7 +291,7 @@ def tile_slru_kernel(tc, inputs, Wi, bi, Wo, bo, params_log, out):
         first(0, 2, 256, 256)
         first(0, 3, 256, 256)
         scan(0, 1, 256, 256)
-        turn("wi1", 3, on_vector=True)
+        turn("wi1", 3)
         scan(0, 2, 256, 256)
         turn("in1", 0)
         turn("in1", 1)
@@ -323,10 +323,10 @@ def tile_slru_kernel(tc, inputs, Wi, bi, Wo, bo, params_log, out):
         scan(1, 3)
         quant_x(0, 0, 512)
         weave(1, 0, 256, "vector")
+        weave(1, 256, 256, "pool")
         scan(2, 0)
         turn("in2", 0)
         turn("in2", 1)
-        weave(1, 256, 256, "scalar")
         scan(2, 1)
         quant("wo0", 0, 1024)
         first(3, 0)

@@ -93,7 +93,6 @@ def tile_slru_kernel(tc, inputs, Wi, bi, Wo, bo, params_log, out):
         gam = const.tile([P, 8], F32, name="gam")
         gb = const.tile([P, 8], F32, name="gb")
         lam_p = ps_c.tile([P, 8], F32, name="lam_p")
-        bo_f = const.tile([P, H], F32, name="bo_f")
 
         def constants():
             nc.scalar.activation(out=nu[:], in_=pl[0][:], func=ACTF.Exp)
@@ -200,8 +199,8 @@ def tile_slru_kernel(tc, inputs, Wi, bi, Wo, bo, params_log, out):
             if lo == 0:
                 t = gpool.tile([P, CH, 4], BF16, name="gx", align_bytes=64)
                 gx[u] = t
-            dst = gx[u][:, lo : lo + n, :]
-            src = xs[u][:, :, lo : lo + n].rearrange("p j t -> p t j")
+            dst = gx[u][:, lo : lo + n, :].rearrange("p (c i) j -> p c j i", i=4)
+            src = xs[u][:, :, lo : lo + n].rearrange("p j (c i) -> p c j i", i=4)
             if engine == "pool":
                 nc.gpsimd.tensor_scalar(
                     out=dst, in0=src, scalar1=1.0, scalar2=0.0, op0=ALU.mult, op1=ALU.add
@@ -245,10 +244,10 @@ def tile_slru_kernel(tc, inputs, Wi, bi, Wo, bo, params_log, out):
             o, acc = outs[c, i], acc2[c, i, h]
             hs = slice(512 * h, 512 * (h + 1))
             if on_vector:
-                nc.vector.tensor_tensor(out=o[:, hs], in0=acc[:], in1=bo_f[:, hs], op=ALU.add)
+                nc.vector.tensor_tensor(out=o[:, hs], in0=acc[:], in1=bo_b[:, hs], op=ALU.add)
             else:
                 nc.scalar.copy(out=o[:, hs], in_=acc[:])
-                nc.gpsimd.tensor_tensor(out=o[:, hs], in0=o[:, hs], in1=bo_f[:, hs], op=ALU.add)
+                nc.gpsimd.tensor_tensor(out=o[:, hs], in0=o[:, hs], in1=bo_b[:, hs], op=ALU.add)
             r0 = c * CH + i * P
             if c == NCH - 1 and i >= 2:
                 nc.sync.dma_start(out=o_out[r0 : r0 + P, hs], in_=o[:, hs])
@@ -303,9 +302,6 @@ def tile_slru_kernel(tc, inputs, Wi, bi, Wo, bo, params_log, out):
         turn("in1", 3)
         first(1, 2)
         first(1, 3)
-        nc.gpsimd.tensor_scalar(
-            out=bo_f[:], in0=bo_b[:], scalar1=1.0, scalar2=0.0, op0=ALU.mult, op1=ALU.add
-        )
         weave(0, 0, 256, "vector")
         scan(1, 0)
         turn("wo0", 0)

@@ -35,6 +35,7 @@ def tile_slru_kernel(tc, inputs, Wi, bi, Wo, bo, params_log, out):
         stg = ctx.enter_context(tc.tile_pool(name="stg", bufs=2))
         vpool = ctx.enter_context(tc.tile_pool(name="vp", bufs=8))
         xpool = ctx.enter_context(tc.tile_pool(name="xp", bufs=3))
+        ppool = ctx.enter_context(tc.tile_pool(name="pp", bufs=2))
         gpool = ctx.enter_context(tc.tile_pool(name="gp", bufs=2))
         opool = ctx.enter_context(tc.tile_pool(name="op", bufs=7))
         psum = ctx.enter_context(tc.psum_pool(name="ps", bufs=7))
@@ -146,7 +147,28 @@ def tile_slru_kernel(tc, inputs, Wi, bi, Wo, bo, params_log, out):
                 in_=stages[nm][:, 2 * lo : 2 * (lo + n)].bitcast(BF16),
             )
 
-        acc1, vs, xs, gx = {}, {}, {}, {}
+        vs, xs, xq, starts, gx = {}, {}, {}, {}, {}
+
+        def final(u, lo, n):
+            return ((u // 2) * CH + lo + n) % SEQ == 0
+
+        def carry(u, j, lo=0):
+            ct = 4 * (u % 2) + j
+            state = xs[u][:, j, lo - 1 : lo] if lo > 0 else xs[u - 2][:, j, CH - 1 : CH]
+            v0 = vs[u, j][:, lo : lo + 1]
+            if u < 6:
+                nc.gpsimd.tensor_scalar(
+                    out=v0,
+                    in0=state,
+                    scalar1=lam[:, ct : ct + 1],
+                    scalar2=v0,
+                    op0=ALU.mult,
+                    op1=ALU.add,
+                )
+            else:
+                nc.scalar.activation(
+                    out=v0, in_=state, func=ACTF.Identity, scale=lam[:, ct : ct + 1], bias=v0
+                )
 
         def first(u, j, lo=0, n=CH):
             c, g2 = u // 2, u % 2
@@ -179,6 +201,20 @@ def tile_slru_kernel(tc, inputs, Wi, bi, Wo, bo, params_log, out):
         def scan(u, j, lo=0, n=CH):
             c, g2 = u // 2, u % 2
             ct = 4 * g2 + j
+            if final(u, lo, n):
+                if j == 0:
+                    t = ppool.tile([P, 2, CH, 2], BF16, name="xpair", align_bytes=64)
+                    xq[u] = t
+                    starts[u] = lo
+                nc.vector.tensor_tensor_scan(
+                    out=xq[u][:, j // 2, lo : lo + n, j % 2],
+                    data0=lam_p[:, ct : ct + 1].to_broadcast([P, n]),
+                    data1=vs[u, j][:, lo : lo + n],
+                    initial=0.0,
+                    op0=ALU.mult,
+                    op1=ALU.add,
+                )
+                return
             if j == 0 and lo == 0:
                 t = xpool.tile([P, 4, CH], F32, name="xs")
                 xs[u] = t
@@ -199,6 +235,16 @@ def tile_slru_kernel(tc, inputs, Wi, bi, Wo, bo, params_log, out):
             if lo == 0:
                 t = gpool.tile([P, CH, 4], BF16, name="gx", align_bytes=64)
                 gx[u] = t
+            if u in xq and lo >= starts[u]:
+                dst = gx[u][:].rearrange("p t j -> p (t j)").bitcast(F32)
+                src = xq[u][:].rearrange("p q t e -> p (q t e)").bitcast(F32)
+                dst = dst.rearrange("p (t q) -> p t q", q=2)[:, lo : lo + n, :]
+                src = src.rearrange("p (q t) -> p t q", q=2)[:, lo : lo + n, :]
+                if engine == "vector":
+                    nc.vector.tensor_copy(out=dst, in_=src)
+                else:
+                    nc.scalar.copy(out=dst, in_=src)
+                return
             dst = gx[u][:, lo : lo + n, :].rearrange("p (c i) j -> p c j i", i=4)
             src = xs[u][:, :, lo : lo + n].rearrange("p j (c i) -> p c j i", i=4)
             if engine == "pool":
@@ -238,7 +284,8 @@ def tile_slru_kernel(tc, inputs, Wi, bi, Wo, bo, params_log, out):
             acc2[c, i, h] = acc
 
         def drain(c, i, h, on_vector):
-            if h == 0:
+            begun = (c, i) in outs
+            if not begun:
                 o = opool.tile([P, H], F32, name="o")
                 outs[c, i] = o
             o, acc = outs[c, i], acc2[c, i, h]
@@ -251,7 +298,7 @@ def tile_slru_kernel(tc, inputs, Wi, bi, Wo, bo, params_log, out):
             r0 = c * CH + i * P
             if c == NCH - 1 and i >= 2:
                 nc.sync.dma_start(out=o_out[r0 : r0 + P, hs], in_=o[:, hs])
-            elif h == 1:
+            elif begun:
                 nc.sync.dma_start(out=o_out[r0 : r0 + P, :], in_=o[:])
 
         turn("in0", 0)
@@ -259,8 +306,8 @@ def tile_slru_kernel(tc, inputs, Wi, bi, Wo, bo, params_log, out):
         for g in range(2):
             quant("in0", 512 * g, 256)
         turn("wi0", 0)
-        turn("wi0", 1, on_vector=True)
         quant("wi0", 0, 256)
+        turn("wi0", 1, on_vector=True)
         turn("wi0", 2)
         constants()
         quant("wi0", 256, 256)
@@ -305,17 +352,21 @@ def tile_slru_kernel(tc, inputs, Wi, bi, Wo, bo, params_log, out):
         weave(0, 0, 256, "vector")
         scan(1, 0)
         turn("wo0", 0)
-        weave(0, 256, 256, "scalar")
+        weave(0, 256, 256, "pool")
         scan(1, 1)
         quant("in1", 0, 1024)
         turn("wo0", 1)
         first(2, 0)
         first(2, 1)
+        carry(2, 0)
+        carry(2, 1)
         scan(1, 2)
         turn("wo0", 2)
         turn("wo0", 3)
         first(2, 2)
         first(2, 3)
+        carry(2, 2)
+        carry(2, 3)
         scan(1, 3)
         quant_x(0, 0, 512)
         weave(1, 0, 256, "vector")
@@ -327,18 +378,21 @@ def tile_slru_kernel(tc, inputs, Wi, bi, Wo, bo, params_log, out):
         quant("wo0", 0, 1024)
         first(3, 0)
         first(3, 1)
+        carry(3, 0)
+        carry(3, 1)
         turn("in2", 2)
         turn("in2", 3)
         scan(2, 2)
         first(3, 2)
         first(3, 3)
+        carry(3, 2)
+        carry(3, 3)
         turn("wo1", 0)
         turn("wo1", 1)
         scan(2, 3)
         quant_x(1, 0, 512)
         turn("wo1", 2)
         turn("wo1", 3)
-        weave(2, 0, 256, "vector")
         rows = [(c, i) for c in range(NCH) for i in range(4)]
         late = []
         for s in range(3, 6):
@@ -350,8 +404,11 @@ def tile_slru_kernel(tc, inputs, Wi, bi, Wo, bo, params_log, out):
                 quant("in3", 0, 1024)
             if s > 3:
                 drain(*late[0], 0, False)
-                drain(*late[0], 1, True)
-            weave(s - 1, 256, 256, "scalar")
+                drain(*late[0], 1, False)
+            if s == 5:
+                weave(4, 256, 256, "scalar")
+            else:
+                weave(s - 1, 0, 512, "scalar")
             first(s + 1, 0)
             first(s + 1, 1)
             scan(s, 1)
@@ -366,6 +423,9 @@ def tile_slru_kernel(tc, inputs, Wi, bi, Wo, bo, params_log, out):
                 turn("in3", 3)
             first(s + 1, 2)
             first(s + 1, 3)
+            if s == 5:
+                for j in range(4):
+                    carry(6, j)
             scan(s, 2)
             drain(*ra, 0, False)
             drain(*ra, 1, True)
@@ -374,77 +434,73 @@ def tile_slru_kernel(tc, inputs, Wi, bi, Wo, bo, params_log, out):
             late = [rb]
             scan(s, 3)
             quant_x(s - 1, 0, 512)
-            weave(s, 0, 256, "pool")
-        scan(6, 0, 0, 256)
+            if s > 3:
+                weave(s, 0, 256, "pool")
+        scan(6, 0)
         drain(1, 1, 0, False)
         drain(1, 1, 1, True)
         first(7, 0)
         first(7, 1)
         weave(5, 256, 256, "scalar")
-        scan(6, 1, 0, 256)
         second(1, 2, 0)
         second(1, 2, 1)
-        scan(6, 2, 0, 256)
+        scan(6, 1)
         first(7, 2)
         first(7, 3)
-        scan(6, 3, 0, 256)
         drain(1, 2, 0, False)
         drain(1, 2, 1, True)
         second(1, 3, 0)
         second(1, 3, 1)
-        scan(7, 0, 0, 256)
-        weave(6, 0, 256, "scalar")
-        scan(7, 1, 0, 256)
+        scan(6, 2)
         quant_x(5, 0, 512)
         second(2, 0, 0)
         second(2, 0, 1)
-        scan(7, 2, 0, 256)
         drain(1, 3, 0, False)
-        drain(1, 3, 1, False)
-        scan(7, 3, 0, 256)
+        drain(1, 3, 1, True)
+        scan(6, 3)
         second(2, 1, 0)
         second(2, 1, 1)
-        weave(7, 0, 256, "scalar")
-        scan(6, 0, 256, 256)
-        quant_x(6, 0, 256)
+        scan(7, 0, 0, 256)
+        weave(6, 0, 512, "scalar")
         drain(2, 0, 0, False)
         drain(2, 0, 1, True)
-        scan(6, 1, 256, 256)
+        scan(7, 1, 0, 256)
         second(2, 2, 0)
         second(2, 2, 1)
         drain(2, 1, 0, False)
         drain(2, 1, 1, True)
-        scan(6, 2, 256, 256)
+        scan(7, 2, 0, 256)
         second(2, 3, 0)
         second(2, 3, 1)
-        scan(6, 3, 256, 256)
-        drain(2, 2, 0, False)
+        scan(7, 3, 0, 256)
+        for j in range(4):
+            carry(7, j, 256)
+        weave(7, 0, 256, "scalar")
         drain(2, 2, 1, True)
-        quant_x(7, 0, 256)
+        quant_x(6, 0, 512)
         scan(7, 0, 256, 256)
-        weave(6, 256, 256, "scalar")
-        drain(2, 3, 0, False)
+        quant_x(7, 0, 256)
+        drain(2, 2, 0, False)
+        scan(7, 1, 256, 256)
         second(3, 0, 0)
         second(3, 0, 1)
-        scan(7, 1, 256, 256)
-        drain(2, 3, 1, True)
+        drain(2, 3, 0, True)
         second(3, 1, 0)
         second(3, 1, 1)
         scan(7, 2, 256, 256)
-        drain(3, 0, 0, True)
+        drain(2, 3, 1, True)
         scan(7, 3, 256, 256)
-        weave(7, 256, 128, "vector")
-        weave(7, 384, 128, "scalar")
-        quant_x(6, 256, 256)
-        quant_x(7, 256, 128)
+        drain(3, 0, 0, False)
         drain(3, 0, 1, True)
+        weave(7, 256, 256, "scalar")
+        drain(3, 1, 1, True)
+        quant_x(7, 256, 256)
+        drain(3, 1, 0, True)
         second(3, 2, 0)
         second(3, 2, 1)
-        quant_x(7, 384, 128)
-        drain(3, 1, 0, True)
-        drain(3, 1, 1, True)
         second(3, 3, 0)
         second(3, 3, 1)
-        for i in range(2, 4):
-            for h in range(2):
-                drain(3, i, h, True)
+        drain(3, 2, 0, True)
+        drain(3, 2, 1, True)
+        drain(3, 3, 0, True)
+        drain(3, 3, 1, True)

@@ -302,193 +302,211 @@ def tile_slru_kernel(tc, inputs, Wi, bi, Wo, bo, params_log, out):
                 nc.sync.dma_start(out=o_out[r0 : r0 + P, :], in_=o[:])
 
         turn("in0", 0)
-        turn("in0", 1, on_vector=True)
+        turn("in0", 1)
+        turn("wi0", 0, on_vector=True)
         for g in range(2):
             quant("in0", 512 * g, 256)
-        turn("wi0", 0)
         quant("wi0", 0, 256)
-        turn("wi0", 1, on_vector=True)
-        turn("wi0", 2)
+        turn("wi0", 1)
         constants()
         quant("wi0", 256, 256)
-        turn("wi0", 3, on_vector=True)
+        turn("wi0", 2, on_vector=True)
+        turn("wi0", 3)
         first(0, 0, 0, 256)
-        turn("in0", 2)
         first(0, 1, 0, 256)
         quant("wi0", 512, 256)
         quant("wi0", 768, 256)
         nc.tensor.matmul(out=lam_p[:], lhsT=ident[:], rhs=lam[:], start=True, stop=True)
         scan(0, 0, 0, 256)
-        turn("in0", 3, on_vector=True)
+        turn("in0", 2)
+        turn("in0", 3)
+        scan(0, 1, 0, 256)
         first(0, 2, 0, 256)
         first(0, 3, 0, 256)
-        scan(0, 1, 0, 256)
         for g in range(2):
             quant("in0", 512 * g + 256, 256)
         turn("wi1", 0)
         scan(0, 2, 0, 256)
         turn("wi1", 1, on_vector=True)
-        first(0, 0, 256, 256)
-        first(0, 1, 256, 256)
+        for j in range(4):
+            first(0, j, 256, 256)
         scan(0, 3, 0, 256)
         quant("wi1", 0, 512)
         turn("wi1", 2)
-        scan(0, 0, 256, 256)
-        first(0, 2, 256, 256)
-        first(0, 3, 256, 256)
-        scan(0, 1, 256, 256)
         turn("wi1", 3)
-        scan(0, 2, 256, 256)
-        turn("in1", 0)
-        turn("in1", 1)
+        weave(0, 0, 256, "vector")
         first(1, 0)
         first(1, 1)
+        scan(0, 0, 256, 256)
+        scan(0, 1, 256, 256)
+        turn("in1", 0)
+        turn("in1", 1)
+        scan(0, 2, 256, 256)
         quant("wi1", 512, 512)
         scan(0, 3, 256, 256)
         turn("in1", 2)
         turn("in1", 3)
         first(1, 2)
         first(1, 3)
-        weave(0, 0, 256, "vector")
         scan(1, 0)
         turn("wo0", 0)
-        weave(0, 256, 256, "pool")
-        scan(1, 1)
-        quant("in1", 0, 1024)
         turn("wo0", 1)
+        scan(1, 1)
+        weave(0, 256, 256, "vector")
+        quant("in1", 0, 1024)
+        turn("wo0", 2)
+        turn("wo0", 3)
         first(2, 0)
         first(2, 1)
         carry(2, 0)
         carry(2, 1)
         scan(1, 2)
-        turn("wo0", 2)
-        turn("wo0", 3)
         first(2, 2)
         first(2, 3)
         carry(2, 2)
         carry(2, 3)
         scan(1, 3)
         quant_x(0, 0, 512)
-        weave(1, 0, 256, "vector")
-        weave(1, 256, 256, "pool")
-        scan(2, 0)
-        turn("in2", 0)
-        turn("in2", 1)
-        scan(2, 1)
         quant("wo0", 0, 1024)
         first(3, 0)
         first(3, 1)
         carry(3, 0)
         carry(3, 1)
-        turn("in2", 2)
-        turn("in2", 3)
-        scan(2, 2)
+        scan(2, 0)
+        weave(1, 0, 256, "vector")
+        weave(1, 256, 256, "vector")
+        turn("in2", 0)
+        turn("in2", 1)
+        scan(2, 1)
         first(3, 2)
         first(3, 3)
         carry(3, 2)
         carry(3, 3)
+        scan(2, 2)
+        turn("in2", 2)
+        turn("in2", 3)
         turn("wo1", 0)
         turn("wo1", 1)
-        scan(2, 3)
-        quant_x(1, 0, 512)
         turn("wo1", 2)
         turn("wo1", 3)
-        rows = [(c, i) for c in range(NCH) for i in range(4)]
-        late = []
-        for s in range(3, 6):
-            ra, rb = rows[2 * s - 6], rows[2 * s - 5]
-            scan(s, 0)
-            if s == 3:
-                quant("in2", 0, 1024)
-            if s == 5:
-                quant("in3", 0, 1024)
-            if s > 3:
-                drain(*late[0], 0, False)
-                drain(*late[0], 1, False)
-            if s == 5:
-                weave(4, 256, 256, "scalar")
-            else:
-                weave(s - 1, 0, 512, "scalar")
-            first(s + 1, 0)
-            first(s + 1, 1)
-            scan(s, 1)
-            if s == 3:
-                quant("wo1", 0, 1024)
-            second(*ra, 0)
-            second(*ra, 1)
-            if s == 4:
-                turn("in3", 0)
-                turn("in3", 1)
-                turn("in3", 2)
-                turn("in3", 3)
-            first(s + 1, 2)
-            first(s + 1, 3)
-            if s == 5:
-                for j in range(4):
-                    carry(6, j)
-            scan(s, 2)
-            drain(*ra, 0, False)
-            drain(*ra, 1, True)
-            second(*rb, 0)
-            second(*rb, 1)
-            late = [rb]
-            scan(s, 3)
-            quant_x(s - 1, 0, 512)
-            if s > 3:
-                weave(s, 0, 256, "pool")
+        scan(2, 3)
+        quant_x(1, 0, 512)
+        quant("in2", 0, 1024)
+        scan(3, 0)
+        weave(2, 0, 512, "scalar")
+        scan(3, 1)
+        quant("wo1", 0, 1024)
+        first(4, 0)
+        first(4, 1)
+        turn("in3", 0)
+        turn("in3", 1)
+        scan(3, 2)
+        second(0, 0, 0)
+        second(0, 0, 1)
+        first(4, 2)
+        first(4, 3)
+        scan(3, 3)
+        drain(0, 0, 0, False)
+        drain(0, 0, 1, False)
+        second(0, 1, 0)
+        second(0, 1, 1)
+        scan(4, 0)
+        turn("in3", 2)
+        turn("in3", 3)
+        weave(3, 0, 512, "scalar")
+        scan(4, 1)
+        drain(0, 1, 0, False)
+        drain(0, 1, 1, False)
+        second(0, 2, 0)
+        second(0, 2, 1)
+        scan(4, 2)
+        quant("in3", 0, 1024)
+        quant_x(2, 0, 512)
+        quant_x(3, 0, 512)
+        first(5, 0)
+        first(5, 1)
+        scan(4, 3)
+        drain(0, 2, 0, False)
+        drain(0, 2, 1, True)
+        second(0, 3, 0)
+        second(0, 3, 1)
+        first(5, 2)
+        first(5, 3)
+        scan(5, 0)
+        weave(4, 0, 256, "pool")
+        weave(4, 256, 256, "scalar")
+        drain(0, 3, 0, False)
+        drain(0, 3, 1, True)
+        first(6, 0)
+        first(6, 1)
+        scan(5, 1)
+        second(1, 0, 0)
+        second(1, 0, 1)
+        first(6, 2)
+        first(6, 3)
+        for j in range(4):
+            carry(6, j)
+        scan(5, 2)
+        drain(1, 0, 0, False)
+        drain(1, 0, 1, True)
+        second(1, 1, 0)
+        second(1, 1, 1)
+        scan(5, 3)
         scan(6, 0)
+        weave(5, 0, 256, "scalar")
+        weave(5, 256, 256, "scalar")
         drain(1, 1, 0, False)
         drain(1, 1, 1, True)
-        first(7, 0)
-        first(7, 1)
-        weave(5, 256, 256, "scalar")
         second(1, 2, 0)
         second(1, 2, 1)
+        first(7, 0)
+        first(7, 1)
         scan(6, 1)
-        first(7, 2)
-        first(7, 3)
         drain(1, 2, 0, False)
         drain(1, 2, 1, True)
         second(1, 3, 0)
         second(1, 3, 1)
+        first(7, 2)
+        first(7, 3)
         scan(6, 2)
+        quant_x(4, 0, 512)
         quant_x(5, 0, 512)
-        second(2, 0, 0)
-        second(2, 0, 1)
+        scan(6, 3)
         drain(1, 3, 0, False)
         drain(1, 3, 1, True)
-        scan(6, 3)
-        second(2, 1, 0)
-        second(2, 1, 1)
+        second(2, 0, 0)
+        second(2, 0, 1)
         scan(7, 0, 0, 256)
         weave(6, 0, 512, "scalar")
+        scan(7, 1, 0, 256)
         drain(2, 0, 0, False)
         drain(2, 0, 1, True)
-        scan(7, 1, 0, 256)
-        second(2, 2, 0)
-        second(2, 2, 1)
+        second(2, 1, 0)
+        second(2, 1, 1)
+        scan(7, 2, 0, 256)
+        scan(7, 3, 0, 256)
         drain(2, 1, 0, False)
         drain(2, 1, 1, True)
-        scan(7, 2, 0, 256)
-        second(2, 3, 0)
-        second(2, 3, 1)
-        scan(7, 3, 0, 256)
+        second(2, 2, 0)
+        second(2, 2, 1)
         for j in range(4):
             carry(7, j, 256)
         weave(7, 0, 256, "scalar")
-        drain(2, 2, 1, True)
-        quant_x(6, 0, 512)
         scan(7, 0, 256, 256)
-        quant_x(7, 0, 256)
         drain(2, 2, 0, False)
+        drain(2, 2, 1, True)
+        second(2, 3, 0)
+        second(2, 3, 1)
+        quant_x(6, 0, 512)
+        quant_x(7, 0, 256)
         scan(7, 1, 256, 256)
+        drain(2, 3, 0, False)
         second(3, 0, 0)
         second(3, 0, 1)
-        drain(2, 3, 0, True)
-        second(3, 1, 0)
-        second(3, 1, 1)
         scan(7, 2, 256, 256)
         drain(2, 3, 1, True)
+        second(3, 1, 0)
+        second(3, 1, 1)
         scan(7, 3, 256, 256)
         drain(3, 0, 0, False)
         drain(3, 0, 1, True)
@@ -500,7 +518,6 @@ def tile_slru_kernel(tc, inputs, Wi, bi, Wo, bo, params_log, out):
         second(3, 2, 1)
         second(3, 3, 0)
         second(3, 3, 1)
-        drain(3, 2, 0, True)
-        drain(3, 2, 1, True)
-        drain(3, 3, 0, True)
-        drain(3, 3, 1, True)
+        for i in range(2, 4):
+            for h in range(2):
+                drain(3, i, h, True)

from contextlib import ExitStack

import concourse.bass as bass
import concourse.mybir as mybir
import concourse.tile as tile
from concourse.masks import make_identity

F32 = mybir.dt.float32
BF16 = mybir.dt.bfloat16
U32 = mybir.dt.uint32
U8 = mybir.dt.uint8
FP8X4 = mybir.dt.float8_e4m3fn_x4
ACTF = mybir.ActivationFunctionType
ALU = mybir.AluOpType

P = 128
TOK = 2048
SEQ = 1024
H = 1024
U = 1024
CH = 512
NCH = TOK // CH

FLOPS = 2 * 2 * TOK * H * U


def tile_slru_kernel(tc, inputs, Wi, bi, Wo, bo, params_log, out):
    nc = tc.nc
    x_in = inputs.flatten_outer_dims()
    o_out = out.flatten_outer_dims()
    with ExitStack() as ctx:
        const = ctx.enter_context(tc.tile_pool(name="const", bufs=1))
        rawp = ctx.enter_context(tc.tile_pool(name="raw", bufs=1))
        keep = ctx.enter_context(tc.tile_pool(name="keep", bufs=1))
        stg = ctx.enter_context(tc.tile_pool(name="stg", bufs=2))
        vpool = ctx.enter_context(tc.tile_pool(name="vp", bufs=8))
        xpool = ctx.enter_context(tc.tile_pool(name="xp", bufs=3))
        ppool = ctx.enter_context(tc.tile_pool(name="pp", bufs=2))
        gpool = ctx.enter_context(tc.tile_pool(name="gp", bufs=2))
        opool = ctx.enter_context(tc.tile_pool(name="op", bufs=7))
        psum = ctx.enter_context(tc.psum_pool(name="ps", bufs=7))
        ps_c = ctx.enter_context(tc.psum_pool(name="psc", bufs=1))
        ctx.enter_context(tc.manual_schedule())

        ident = const.tile([P, P], F32, name="ident")
        make_identity(nc, ident[:])

        raw = {}
        for nm in ("in0", "in1", "in2", "in3", "wi0", "wi1", "wo0", "wo1"):
            t = rawp.tile([P, 4, H], BF16, name="raw_" + nm)
            raw[nm] = t

        def source(nm):
            i = int(nm[2])
            if nm[:2] == "in":
                return x_in[i * CH : (i + 1) * CH, :].rearrange("(i p) h -> p i h", p=P)
            if nm[:2] == "wi":
                return Wi[i * 512 : (i + 1) * 512, :].rearrange("(m e) h -> m e h", e=4)
            return Wo[i * 512 : (i + 1) * 512, :].rearrange("(i p) u -> p i u", p=P)

        def load(nm, pieces, i0=0, i1=None):
            src = source(nm)
            n = 4 // pieces
            for i in range(i0, pieces if i1 is None else i1):
                nc.sync.dma_start(
                    out=raw[nm][:, n * i : n * (i + 1), :], in_=src[:, n * i : n * (i + 1), :]
                )

        pl = [const.tile([P, 8], BF16, name="pl%d" % r) for r in range(2)]
        bi_b = const.tile([P, 8], BF16, name="bi_b")
        load("in0", 4, 0, 2)
        load("wi0", 4)
        for r in range(2):
            nc.sync.dma_start(
                out=pl[r][:].rearrange("m (a e) -> m a e", e=4),
                in_=params_log[r].rearrange("(a m e) -> m a e", a=2, e=4),
            )
        nc.sync.dma_start(
            out=bi_b[:].rearrange("m (a e) -> m a e", e=4),
            in_=bi.rearrange("(a m e) -> m a e", a=2, e=4),
        )
        load("in0", 4, 2, 4)
        load("wi1", 2)
        load("in1", 2)
        load("wo0", 1)
        load("wo1", 1)
        bo_b = const.tile([P, H], BF16, name="bo_b")
        nc.sync.dma_start(out=bo_b[:], in_=bo.partition_broadcast(P))
        load("in2", 1)
        load("in3", 1)

        nu = const.tile([P, 8], F32, name="nu")
        lam = const.tile([P, 8], F32, name="lam")
        gam = const.tile([P, 8], F32, name="gam")
        gb = const.tile([P, 8], F32, name="gb")
        lam_p = ps_c.tile([P, 8], F32, name="lam_p")

        def constants():
            nc.scalar.activation(out=nu[:], in_=pl[0][:], func=ACTF.Exp)
            nc.scalar.activation(out=lam[:], in_=nu[:], func=ACTF.Exp, scale=-1.0)
            nc.scalar.activation(out=gam[:], in_=pl[1][:], func=ACTF.Exp)
            nc.gpsimd.tensor_tensor(out=gb[:], in0=gam[:], in1=bi_b[:], op=ALU.mult)

        codes, scales = {}, {}
        for nm in raw:
            c_t = keep.tile([P, 1024], U32, name="c_" + nm, align_bytes=64)
            s_t = keep.tile([P, 1024], U8, name="s_" + nm, align_bytes=64)
            codes[nm], scales[nm] = c_t, s_t
        xc, xsc = {}, {}
        for c in range(NCH):
            for g in range(2):
                c_t = keep.tile([P, CH], U32, name="xc%d%d" % (c, g), align_bytes=64)
                s_t = keep.tile([P, CH], U8, name="xs%d%d" % (c, g), align_bytes=64)
                xc[c, g], xsc[c, g] = c_t, s_t

        stages = {}

        def turn(nm, i, on_vector=False):
            if i == 0:
                stage = stg.tile([P, 2048], F32, name="stage", align_bytes=64)
                stages[nm] = stage
            bank = psum.tile([P, 2, 2, P], F32, name="bank", tag="bank")
            words = raw[nm][:, i, :].bitcast(F32)
            for g in range(2):
                for u in range(2):
                    nc.tensor.transpose(
                        bank[:, g, u, :], words[:, 256 * g + u : 256 * (g + 1) : 2], ident[:]
                    )
            if nm[:2] == "wi":
                dst = stages[nm][:, 512 * i : 512 * (i + 1)].rearrange(
                    "p (g c u) -> p g c u", g=2, u=2
                )
            else:
                dst = stages[nm][:].rearrange("p (g c u) -> p g c u", g=2, u=2)[
                    :, :, P * i : P * (i + 1), :
                ]
            src = bank[:].rearrange("p g u c -> p g c u")
            if on_vector:
                nc.vector.tensor_copy(out=dst, in_=src)
            else:
                nc.scalar.copy(out=dst, in_=src)

        def quant(nm, lo, n):
            nc.vector.quantize_mx(
                out=codes[nm][:, lo : lo + n].bitcast(FP8X4),
                scales=scales[nm][:, lo : lo + n],
                in_=stages[nm][:, 2 * lo : 2 * (lo + n)].bitcast(BF16),
            )

        vs, xs, xq, starts, gx = {}, {}, {}, {}, {}

        def final(u, lo, n):
            return ((u // 2) * CH + lo + n) % SEQ == 0

        def carry(u, j, lo=0):
            ct = 4 * (u % 2) + j
            state = xs[u][:, j, lo - 1 : lo] if lo > 0 else xs[u - 2][:, j, CH - 1 : CH]
            v0 = vs[u, j][:, lo : lo + 1]
            if u < 6:
                nc.gpsimd.tensor_scalar(
                    out=v0,
                    in0=state,
                    scalar1=lam[:, ct : ct + 1],
                    scalar2=v0,
                    op0=ALU.mult,
                    op1=ALU.add,
                )
            else:
                nc.scalar.activation(
                    out=v0, in_=state, func=ACTF.Identity, scale=lam[:, ct : ct + 1], bias=v0
                )

        def first(u, j, lo=0, n=CH):
            c, g2 = u // 2, u % 2
            ct = 4 * g2 + j
            acc = psum.tile([P, n], F32, name="acc1", tag="bank")
            wi, xi = "wi%d" % g2, "in%d" % c
            for g in range(2):
                w = slice(256 * j + 128 * g, 256 * j + 128 * (g + 1))
                r = slice(512 * g + lo, 512 * g + lo + n)
                nc.tensor.matmul_mx(
                    out=acc[:],
                    lhsT=codes[wi][:, w].bitcast(FP8X4),
                    lhsT_scale=scales[wi][:, w],
                    rhs=codes[xi][:, r].bitcast(FP8X4),
                    rhs_scale=scales[xi][:, r],
                    start=(g == 0),
                    stop=(g == 1),
                )
            if lo == 0:
                v = vpool.tile([P, CH], F32, name="v")
                vs[u, j] = v
            nc.scalar.activation(
                out=vs[u, j][:, lo : lo + n],
                in_=acc[:],
                func=ACTF.Identity,
                scale=gam[:, ct : ct + 1],
                bias=gb[:, ct : ct + 1],
            )

        def scan(u, j, lo=0, n=CH):
            c, g2 = u // 2, u % 2
            ct = 4 * g2 + j
            if final(u, lo, n):
                if j == 0:
                    t = ppool.tile([P, 2, CH, 2], BF16, name="xpair", align_bytes=64)
                    xq[u] = t
                    starts[u] = lo
                nc.vector.tensor_tensor_scan(
                    out=xq[u][:, j // 2, lo : lo + n, j % 2],
                    data0=lam_p[:, ct : ct + 1].to_broadcast([P, n]),
                    data1=vs[u, j][:, lo : lo + n],
                    initial=0.0,
                    op0=ALU.mult,
                    op1=ALU.add,
                )
                return
            if j == 0 and lo == 0:
                t = xpool.tile([P, 4, CH], F32, name="xs")
                xs[u] = t
            if lo > 0:
                init = xs[u][:, j, lo - 1 : lo]
            else:
                init = 0.0 if (c * CH) % SEQ == 0 else xs[u - 2][:, j, CH - 1 : CH]
            nc.vector.tensor_tensor_scan(
                out=xs[u][:, j, lo : lo + n],
                data0=lam_p[:, ct : ct + 1].to_broadcast([P, n]),
                data1=vs[u, j][:, lo : lo + n],
                initial=init,
                op0=ALU.mult,
                op1=ALU.add,
            )

        def weave(u, lo, n, engine):
            if lo == 0:
                t = gpool.tile([P, CH, 4], BF16, name="gx", align_bytes=64)
                gx[u] = t
            if u in xq and lo >= starts[u]:
                dst = gx[u][:].rearrange("p t j -> p (t j)").bitcast(F32)
                src = xq[u][:].rearrange("p q t e -> p (q t e)").bitcast(F32)
                dst = dst.rearrange("p (t q) -> p t q", q=2)[:, lo : lo + n, :]
                src = src.rearrange("p (q t) -> p t q", q=2)[:, lo : lo + n, :]
                if engine == "vector":
                    nc.vector.tensor_copy(out=dst, in_=src)
                else:
                    nc.scalar.copy(out=dst, in_=src)
                return
            dst = gx[u][:, lo : lo + n, :].rearrange("p (c i) j -> p c j i", i=4)
            src = xs[u][:, :, lo : lo + n].rearrange("p j (c i) -> p c j i", i=4)
            if engine == "pool":
                nc.gpsimd.tensor_scalar(
                    out=dst, in0=src, scalar1=1.0, scalar2=0.0, op0=ALU.mult, op1=ALU.add
                )
            elif engine == "vector":
                nc.vector.tensor_copy(out=dst, in_=src)
            else:
                nc.scalar.copy(out=dst, in_=src)

        def quant_x(u, lo, n):
            c, g2 = u // 2, u % 2
            nc.vector.quantize_mx(
                out=xc[c, g2][:, lo : lo + n].bitcast(FP8X4),
                scales=xsc[c, g2][:, lo : lo + n],
                in_=gx[u][:, lo : lo + n, :].rearrange("p t j -> p (t j)"),
            )

        outs, acc2 = {}, {}

        def second(c, i, h):
            acc = psum.tile([P, 512], F32, name="acc2", tag="bank")
            ts = slice(P * i, P * (i + 1))
            wo = "wo%d" % h
            for g in range(2):
                r = slice(512 * g, 512 * (g + 1))
                nc.tensor.matmul_mx(
                    out=acc[:],
                    lhsT=xc[c, g][:, ts].bitcast(FP8X4),
                    lhsT_scale=xsc[c, g][:, ts],
                    rhs=codes[wo][:, r].bitcast(FP8X4),
                    rhs_scale=scales[wo][:, r],
                    start=(g == 0),
                    stop=(g == 1),
                )
            acc2[c, i, h] = acc

        def drain(c, i, h, on_vector):
            begun = (c, i) in outs
            if not begun:
                o = opool.tile([P, H], F32, name="o")
                outs[c, i] = o
            o, acc = outs[c, i], acc2[c, i, h]
            hs = slice(512 * h, 512 * (h + 1))
            if on_vector:
                nc.vector.tensor_tensor(out=o[:, hs], in0=acc[:], in1=bo_b[:, hs], op=ALU.add)
            else:
                nc.scalar.copy(out=o[:, hs], in_=acc[:])
                nc.gpsimd.tensor_tensor(out=o[:, hs], in0=o[:, hs], in1=bo_b[:, hs], op=ALU.add)
            r0 = c * CH + i * P
            if c == NCH - 1 and i >= 2:
                nc.sync.dma_start(out=o_out[r0 : r0 + P, hs], in_=o[:, hs])
            elif begun:
                nc.sync.dma_start(out=o_out[r0 : r0 + P, :], in_=o[:])

        turn("in0", 0)
        turn("in0", 1)
        turn("wi0", 0, on_vector=True)
        for g in range(2):
            quant("in0", 512 * g, 256)
        quant("wi0", 0, 256)
        turn("wi0", 1)
        constants()
        quant("wi0", 256, 256)
        turn("wi0", 2, on_vector=True)
        turn("wi0", 3)
        first(0, 0, 0, 256)
        first(0, 1, 0, 256)
        quant("wi0", 512, 256)
        quant("wi0", 768, 256)
        nc.tensor.matmul(out=lam_p[:], lhsT=ident[:], rhs=lam[:], start=True, stop=True)
        scan(0, 0, 0, 256)
        turn("in0", 2)
        turn("in0", 3)
        scan(0, 1, 0, 256)
        first(0, 2, 0, 256)
        first(0, 3, 0, 256)
        for g in range(2):
            quant("in0", 512 * g + 256, 256)
        turn("wi1", 0)
        scan(0, 2, 0, 256)
        turn("wi1", 1, on_vector=True)
        for j in range(4):
            first(0, j, 256, 256)
        scan(0, 3, 0, 256)
        quant("wi1", 0, 512)
        turn("wi1", 2)
        turn("wi1", 3)
        weave(0, 0, 256, "vector")
        first(1, 0)
        first(1, 1)
        scan(0, 0, 256, 256)
        scan(0, 1, 256, 256)
        turn("in1", 0)
        turn("in1", 1)
        scan(0, 2, 256, 256)
        quant("wi1", 512, 512)
        scan(0, 3, 256, 256)
        turn("in1", 2)
        turn("in1", 3)
        first(1, 2)
        first(1, 3)
        scan(1, 0)
        turn("wo0", 0)
        turn("wo0", 1)
        scan(1, 1)
        weave(0, 256, 256, "vector")
        quant("in1", 0, 1024)
        turn("wo0", 2)
        turn("wo0", 3)
        first(2, 0)
        first(2, 1)
        carry(2, 0)
        carry(2, 1)
        scan(1, 2)
        first(2, 2)
        first(2, 3)
        carry(2, 2)
        carry(2, 3)
        scan(1, 3)
        quant_x(0, 0, 512)
        quant("wo0", 0, 1024)
        first(3, 0)
        first(3, 1)
        carry(3, 0)
        carry(3, 1)
        scan(2, 0)
        weave(1, 0, 256, "vector")
        weave(1, 256, 256, "vector")
        turn("in2", 0)
        turn("in2", 1)
        scan(2, 1)
        first(3, 2)
        first(3, 3)
        carry(3, 2)
        carry(3, 3)
        scan(2, 2)
        turn("in2", 2)
        turn("in2", 3)
        turn("wo1", 0)
        turn("wo1", 1)
        turn("wo1", 2)
        turn("wo1", 3)
        scan(2, 3)
        quant_x(1, 0, 512)
        quant("in2", 0, 1024)
        scan(3, 0)
        weave(2, 0, 512, "scalar")
        scan(3, 1)
        quant("wo1", 0, 1024)
        first(4, 0)
        first(4, 1)
        turn("in3", 0)
        turn("in3", 1)
        scan(3, 2)
        second(0, 0, 0)
        second(0, 0, 1)
        first(4, 2)
        first(4, 3)
        scan(3, 3)
        drain(0, 0, 0, False)
        drain(0, 0, 1, False)
        second(0, 1, 0)
        second(0, 1, 1)
        scan(4, 0)
        turn("in3", 2)
        turn("in3", 3)
        weave(3, 0, 512, "scalar")
        scan(4, 1)
        drain(0, 1, 0, False)
        drain(0, 1, 1, False)
        second(0, 2, 0)
        second(0, 2, 1)
        scan(4, 2)
        quant("in3", 0, 1024)
        quant_x(2, 0, 512)
        quant_x(3, 0, 512)
        first(5, 0)
        first(5, 1)
        scan(4, 3)
        drain(0, 2, 0, False)
        drain(0, 2, 1, True)
        second(0, 3, 0)
        second(0, 3, 1)
        first(5, 2)
        first(5, 3)
        scan(5, 0)
        weave(4, 0, 256, "pool")
        weave(4, 256, 256, "scalar")
        drain(0, 3, 0, False)
        drain(0, 3, 1, True)
        first(6, 0)
        first(6, 1)
        scan(5, 1)
        second(1, 0, 0)
        second(1, 0, 1)
        first(6, 2)
        first(6, 3)
        for j in range(4):
            carry(6, j)
        scan(5, 2)
        drain(1, 0, 0, False)
        drain(1, 0, 1, True)
        second(1, 1, 0)
        second(1, 1, 1)
        scan(5, 3)
        scan(6, 0)
        weave(5, 0, 256, "scalar")
        weave(5, 256, 256, "scalar")
        drain(1, 1, 0, False)
        drain(1, 1, 1, True)
        second(1, 2, 0)
        second(1, 2, 1)
        first(7, 0)
        first(7, 1)
        scan(6, 1)
        drain(1, 2, 0, False)
        drain(1, 2, 1, True)
        second(1, 3, 0)
        second(1, 3, 1)
        first(7, 2)
        first(7, 3)
        scan(6, 2)
        quant_x(4, 0, 512)
        quant_x(5, 0, 512)
        scan(6, 3)
        drain(1, 3, 0, False)
        drain(1, 3, 1, True)
        second(2, 0, 0)
        second(2, 0, 1)
        scan(7, 0, 0, 256)
        weave(6, 0, 512, "scalar")
        scan(7, 1, 0, 256)
        drain(2, 0, 0, False)
        drain(2, 0, 1, True)
        second(2, 1, 0)
        second(2, 1, 1)
        scan(7, 2, 0, 256)
        scan(7, 3, 0, 256)
        drain(2, 1, 0, False)
        drain(2, 1, 1, True)
        second(2, 2, 0)
        second(2, 2, 1)
        for j in range(4):
            carry(7, j, 256)
        weave(7, 0, 256, "scalar")
        scan(7, 0, 256, 256)
        drain(2, 2, 0, False)
        drain(2, 2, 1, True)
        second(2, 3, 0)
        second(2, 3, 1)
        quant_x(6, 0, 512)
        quant_x(7, 0, 256)
        scan(7, 1, 256, 256)
        drain(2, 3, 0, False)
        second(3, 0, 0)
        second(3, 0, 1)
        scan(7, 2, 256, 256)
        drain(2, 3, 1, True)
        second(3, 1, 0)
        second(3, 1, 1)
        scan(7, 3, 256, 256)
        drain(3, 0, 0, False)
        drain(3, 0, 1, True)
        weave(7, 256, 256, "scalar")
        drain(3, 1, 1, True)
        quant_x(7, 256, 256)
        drain(3, 1, 0, True)
        second(3, 2, 0)
        second(3, 2, 1)
        second(3, 3, 0)
        second(3, 3, 1)
        for i in range(2, 4):
            for h in range(2):
                drain(3, i, h, True)
